import numpy as np
import ml_dtypes


def mxq(x, axis, fmt="e4m3"):
    dtype, down = {"e4m3": (ml_dtypes.float8_e4m3fn, 7), "e5m2": (ml_dtypes.float8_e5m2, 14)}[fmt]
    v = np.moveaxis(np.asarray(x, np.float32).astype(ml_dtypes.bfloat16).astype(np.float64), axis, -1)
    blocks = v.reshape(v.shape[:-1] + (-1, 32))
    amax = np.abs(blocks).max(-1, keepdims=True)
    byte = np.maximum(np.where(amax > 0, np.frexp(amax)[1] - 1 + 127, 0) - down, 1)
    scale = np.exp2(byte - 127.0)
    codes = (blocks / scale).astype(np.float32).astype(dtype).astype(np.float64)
    return np.moveaxis((codes * scale).reshape(v.shape), -1, axis)


WIDE = False


def mx_kscale(k):
    if not WIDE:
        return np.ones(k)
    levels = np.array([10, -10, 5, -5, 0])
    if k % 512:
        return np.exp2(np.random.permutation(np.resize(levels, k // 32))).repeat(32)
    a = np.empty((k // 512, 16))
    for p in range(k // 512):
        a[p, :8] = np.random.permutation(np.resize(levels, 8))
        for g in range(8):
            far = levels[np.abs(levels - a[p, g]) >= 10]
            a[p, g + 8] = far[np.random.randint(len(far))]
    return np.exp2(a.ravel()).repeat(32)


BF16 = ml_dtypes.bfloat16


def bf(x):
    return np.asarray(x, np.float32).astype(BF16)


def f64(x):
    return np.asarray(x).astype(np.float64)


B, S, H, A, NH = 4, 128, 1536, 1536, 12
HD = A // NH
LN_EPS = 1e-5


def draw0():
    s = mx_kscale(A)
    return {"ctx_heads": bf(np.random.standard_normal((B, NH, S, HD)) * s.reshape(NH, 1, HD)),
            "Wo": bf(np.random.standard_normal((H, A)) / np.sqrt(A) / s),
            "bo": bf(np.random.standard_normal(H) * 0.3),
            "features": bf(np.random.standard_normal((B, S, H))),
            "ln_g": bf(1.0 + 0.1 * np.random.standard_normal(H)),
            "ln_b": bf(0.2 * np.random.standard_normal(H))}


def core(ctx_heads, Wo, bo, features, ln_g, ln_b):
    ctx = f64(ctx_heads).transpose(0, 2, 1, 3).reshape(B, S, A)
    p = (mxq(ctx, 2, "e4m3") @ mxq(f64(Wo), 1, "e4m3").T) + f64(bo)
    y = p + f64(features)
    mu = y.mean(-1, keepdims=True)
    var = y.var(-1, keepdims=True)
    return (y - mu) / np.sqrt(var + LN_EPS) * f64(ln_g) + f64(ln_b)


def e4m3fn_bytes(y):
    return np.clip(np.asarray(y, np.float64), -448.0, 448.0).astype(np.float32).astype(ml_dtypes.float8_e4m3fn).view(np.uint8)


def e4m3fn_values(b):
    return np.asarray(b, np.uint8).view(ml_dtypes.float8_e4m3fn).astype(np.float64)


def setup_inputs():
    d = draw0()
    x0 = np.asarray(d['Wo']).astype(np.float64)
    s = (np.max(np.abs(x0), axis=(0,), keepdims=True) / 448.0).astype(np.float32)
    out = {}
    for k, v in d.items():
        if k == 'Wo':
            out['Wo_bytes'] = e4m3fn_bytes(x0 / s.astype(np.float64))
            out['Wo_scale'] = s
        else:
            out[k] = v
    return out


def reference(ctx_heads, Wo_bytes, Wo_scale, bo, features, ln_g, ln_b):
    return core(ctx_heads, e4m3fn_values(Wo_bytes) * Wo_scale.astype(np.float64), bo, features, ln_g, ln_b)

@@ -1,0 +1,309 @@
+from contextlib import ExitStack
+
+import concourse.mybir as mybir
+from concourse.masks import make_identity
+
+FLOPS = 2 * 512 * 1536 * 1536
+
+F32 = mybir.dt.float32
+BF16 = mybir.dt.bfloat16
+U32 = mybir.dt.uint32
+U8 = mybir.dt.uint8
+FP8 = mybir.dt.float8_e4m3fn
+FP8X4 = mybir.dt.float8_e4m3fn_x4
+ALU = mybir.AluOpType
+ACT = mybir.ActivationFunctionType
+AX = mybir.AxisListType
+
+P = 128
+K = 1536
+N = 1536
+NB = 4
+PASSES = 3
+LN_EPS = 1e-5
+
+
+def tile_hierarchicalattention_pb_kernel(tc, ctx_heads, Wo_bytes, Wo_scale, bo, features, ln_g, ln_b, out):
+    nc = tc.nc
+    with ExitStack() as es:
+        const = es.enter_context(tc.tile_pool(name="const", bufs=1))
+        wbf_pool = es.enter_context(tc.tile_pool(name="wbf", bufs=6))
+        grp_pool = es.enter_context(tc.tile_pool(name="grp", bufs=3))
+        tp_pool = es.enter_context(tc.psum_pool(name="tp", bufs=3))
+        acc_pool = es.enter_context(tc.psum_pool(name="acc", bufs=2))
+        y_pool = es.enter_context(tc.psum_pool(name="yps", bufs=3))
+        es.enter_context(tc.manual_schedule())
+
+        ident = const.tile([P, P], F32, name="ident")
+        warm = const.tile([P, 1], F32, name="warm")
+        ones = const.tile([P, 256], F32, name="ones")
+        scale_part = [const.tile([P, 512], F32, name="scale_part%d" % g) for g in range(PASSES)]
+        scale_bc = const.tile([P, K], F32, name="scale_bc")
+        bo_col = const.tile([P, 12], BF16, name="bo_col")
+        g_bc = const.tile([P, N], BF16, name="g_bc")
+        b_bc = const.tile([P, N], BF16, name="b_bc")
+        wo_raw = [const.tile([P, K], U8, name="wo_raw%d" % j) for j in range(12)]
+        ctx_sb = [const.tile([P, 2, K], BF16, name="ctx_sb%d" % bp) for bp in range(2)]
+        cgrp = const.tile([P, PASSES * 2048], BF16, name="cgrp", align_bytes=64)
+        ctx_codes = const.tile([P, PASSES * 512], U32, name="ctx_codes", align_bytes=64)
+        ctx_sc = const.tile([P, PASSES * 512], U8, name="ctx_sc", align_bytes=64)
+        wo_codes = [[const.tile([P, 256 * w], U32, name="wo_codes%d_%d" % (q, w), align_bytes=64) for w in (2, 1)]
+                    for q in range(6)]
+        wo_sc = [[const.tile([P, 256 * w], U8, name="wo_sc%d_%d" % (q, w), align_bytes=64) for w in (2, 1)]
+                 for q in range(6)]
+        a_t = [const.tile([P, 512], F32, name="a_t%d" % j) for j in range(12)]
+        feat = [const.tile([P, N], BF16, name="feat%d" % b) for b in range(NB)]
+        fy = [const.tile([P, N], F32, name="fy%d" % b) for b in range(NB)]
+        zt = [const.tile([P, N], F32, name="zt%d" % b) for b in range(NB)]
+        junk = const.tile([P, N], BF16, name="junk")
+        sums = const.tile([P, NB, 3], F32, name="sums")
+        tot = const.tile([P, NB, 3], F32, name="tot")
+        negmu = const.tile([P, NB], F32, name="negmu")
+        ssq = const.tile([P, NB], F32, name="ssq")
+        rstd = const.tile([P, NB], F32, name="rstd")
+
+        scale_row = Wo_scale.rearrange("o k -> (o k)")
+        def load_scale(queue, g):
+            queue.dma_start(out=scale_part[g][:], in_=scale_row[512 * g:512 * (g + 1)].partition_broadcast(P))
+
+        def load_wo(j):
+            nc.sync.dma_start(out=wo_raw[j][:], in_=Wo_bytes[P * j:P * (j + 1), :])
+
+        def load_ctx(bp):
+            nc.sync.dma_start(out=ctx_sb[bp][:].rearrange("p b (h d) -> p (b h) d", h=12),
+                              in_=ctx_heads[2 * bp:2 * bp + 2].rearrange("b h s d -> s (b h) d"))
+
+        load_scale(nc.scalar, 0)
+        load_scale(nc.scalar, 2)
+        load_wo(0)
+        load_scale(nc.sync, 1)
+        for j in range(1, 4):
+            load_wo(j)
+        load_ctx(0)
+        for j in range(4, 7):
+            load_wo(j)
+        load_ctx(1)
+        for j in range(7, 12):
+            load_wo(j)
+        for b in range(NB):
+            nc.sync.dma_start(out=feat[b][:], in_=features[b])
+        nc.sync.dma_start(out=g_bc[:], in_=ln_g.partition_broadcast(P))
+        nc.sync.dma_start(out=b_bc[:], in_=ln_b.partition_broadcast(P))
+        make_identity(nc, ident[:])
+        with nc.allow_non_contiguous_dma(reason="one bias value to a partition"):
+            nc.gpsimd.dma_start(out=bo_col[:], in_=bo.rearrange("(j p) -> p j", p=P))
+        nc.vector.memset(warm[:], 1.0)
+        nc.vector.memset(ones[:], 1.0)
+        nc.scalar.activation(out=warm[:], in_=warm[:], func=ACT.Abs_reciprocal_sqrt)
+
+        def keep_busy(words):
+            scratch = y_pool.tile([P, 512], F32, name="yps", tag="yps")
+            nc.tensor.matmul(out=scratch[:, 0:256], lhsT=ident[:], rhs=words, start=True, stop=True)
+
+        def new_pair():
+            two = [wbf_pool.tile([P, K], BF16, name="wbf", tag="wbf") for i in range(2)]
+            return [two[0][:], two[1][:]]
+
+        def widen(q, two, pieces):
+            for i, g in pieces:
+                cols = slice(0, K) if g is None else slice(512 * g, 512 * (g + 1))
+                nc.vector.tensor_tensor(out=two[i][:, cols], in0=wo_raw[2 * q + i][:, cols].bitcast(FP8),
+                                        in1=(scale_part[g][:] if q == 0 else scale_bc[:, cols]), op=ALU.mult)
+
+        def turn_bank(two, g):
+            bank = tp_pool.tile([P, 2, 2, P], F32, name="tp", tag="tp")
+            for i in range(2):
+                words = two[i].bitcast(F32)
+                for u in range(2):
+                    nc.tensor.transpose(out=bank[:, i, u, :], in_=words[:, 256 * g + u:256 * (g + 1):2],
+                                        identity=ident[:])
+            return bank
+
+        def turn(two):
+            return [turn_bank(two, g) for g in range(PASSES)]
+
+        def copy_out(bank, dst_words):
+            nc.scalar.copy(out=dst_words.rearrange("p (i r u) -> p i r u", i=2, u=2),
+                           in_=bank[:].rearrange("p i u r -> p i r u"))
+
+        def ctx_turn(bp):
+            banks = turn([ctx_sb[bp][:, 0, :], ctx_sb[bp][:, 1, :]])
+            for g in range(PASSES):
+                copy_out(banks[g], cgrp[:].bitcast(F32)[:, 1024 * g + 512 * bp:1024 * g + 512 * (bp + 1)])
+
+        def ctx_quant():
+            for lo, hi in ((0, 2), (2, 3)):
+                nc.vector.quantize_mx(out=ctx_codes[:, 512 * lo:512 * hi].bitcast(FP8X4),
+                                      scales=ctx_sc[:, 512 * lo:512 * hi], in_=cgrp[:, 2048 * lo:2048 * hi])
+
+        def new_grp():
+            return [grp_pool.tile([P, 2048], BF16, name="grp_a", tag="grp_a", align_bytes=64),
+                    grp_pool.tile([P, 1024], BF16, name="grp_b", tag="grp_b", align_bytes=64)]
+
+        def wo_turn_pass(two, grp, g):
+            bank = turn_bank(two, g)
+            copy_out(bank, grp[g // 2][:].bitcast(F32)[:, 512 * (g % 2):512 * (g % 2 + 1)])
+
+        def wo_turn(two):
+            grp = new_grp()
+            for g in range(PASSES):
+                wo_turn_pass(two, grp, g)
+            return grp
+
+        def wo_quant(q, grp, parts):
+            for part in parts:
+                nc.vector.quantize_mx(out=wo_codes[q][part][:].bitcast(FP8X4), scales=wo_sc[q][part][:],
+                                      in_=grp[part][:])
+
+        def new_accs():
+            return [acc_pool.tile([P, 512], F32, name="acc", tag="acc") for i in range(2)]
+
+        def multiply(q, accs, steps):
+            for i, g in steps:
+                rows = slice(256 * (g % 2) + P * i, 256 * (g % 2) + P * (i + 1))
+                toks = slice(512 * g, 512 * (g + 1))
+                nc.tensor.matmul_mx(out=accs[i][:],
+                                    lhsT=wo_codes[q][g // 2][:, rows].bitcast(FP8X4),
+                                    lhsT_scale=wo_sc[q][g // 2][:, rows],
+                                    rhs=ctx_codes[:, toks].bitcast(FP8X4), rhs_scale=ctx_sc[:, toks],
+                                    start=(g == 0), stop=(g == PASSES - 1))
+
+        def evacuate_one(q, accs, i):
+            j = 2 * q + i
+            nc.scalar.activation(out=a_t[j][:], in_=accs[i][:], func=ACT.Identity, bias=bo_col[:, j:j + 1],
+                                 scale=1.0)
+
+        def evacuate(q, accs):
+            for i in range(2):
+                evacuate_one(q, accs, i)
+
+        def turn_back(J, b):
+            ybank = y_pool.tile([P, 512], F32, name="yps", tag="yps")
+            for i in range(4):
+                nc.tensor.transpose(out=ybank[:, P * i:P * (i + 1)], in_=a_t[4 * J + i][:, P * b:P * (b + 1)],
+                                    identity=ident[:])
+            return ybank
+
+        def add_residual(J, b, ybank):
+            cols = slice(512 * J, 512 * (J + 1))
+            nc.vector.scalar_tensor_tensor(out=fy[b][:, cols], in0=ybank[:], scalar=1.0, in1=feat[b][:, cols],
+                                           op0=ALU.mult, op1=ALU.add, accum_out=sums[:, b, J:J + 1])
+
+        every = [(i, g) for i in range(2) for g in range(PASSES)]
+        both = [0, 1]
+        grps = {}
+
+        def product(q):
+            accs = new_accs()
+            multiply(q, accs, every)
+            evacuate(q, accs)
+
+        def words_of(tile_ap, g):
+            return tile_ap.bitcast(F32)[:, 256 * g:256 * (g + 1)]
+
+        for n in range(3):
+            keep_busy(ones[:])
+        w = new_pair()
+        widen(0, w, [(0, 0), (0, 1), (1, 0), (1, 1), (0, 2), (1, 2)])
+        for g in range(PASSES):
+            nc.scalar.copy(out=scale_bc[:, 512 * g:512 * (g + 1)], in_=scale_part[g][:])
+        grps[0] = new_grp()
+        for g in range(PASSES):
+            wo_turn_pass(w, grps[0], g)
+            keep_busy(words_of(w[1], g))
+        w = new_pair()
+        widen(1, w, [(0, None)])
+        keep_busy(words_of(w[0], 0))
+        widen(1, w, [(1, None)])
+        ctx_turn(0)
+        keep_busy(words_of(w[1], 0))
+        grps[1] = wo_turn(w)
+        wo_quant(0, grps[0], both)
+        w = new_pair()
+        widen(2, w, [(0, None)])
+        keep_busy(words_of(w[0], 0))
+        widen(2, w, [(1, None)])
+        grps[2] = wo_turn(w)
+        keep_busy(words_of(w[1], 0))
+        wo_quant(1, grps[1], both)
+        ctx_turn(1)
+        w = new_pair()
+        widen(3, w, [(0, None)])
+        keep_busy(words_of(w[0], 0))
+        widen(3, w, [(1, None)])
+        grps[3] = wo_turn(w)
+        ctx_quant()
+        wo_quant(2, grps[2], both)
+        product(0)
+        product(1)
+        product(2)
+        w = new_pair()
+        widen(4, w, [(0, None), (1, None)])
+        grps[4] = wo_turn(w)
+        wo_quant(3, grps[3], both)
+        accs = new_accs()
+        multiply(3, accs, every[0:3])
+        evacuate_one(3, accs, 0)
+        w = new_pair()
+        widen(5, w, [(i, g) for g in range(PASSES) for i in range(2)])
+        grps[5] = new_grp()
+        wo_turn_pass(w, grps[5], 0)
+        wo_turn_pass(w, grps[5], 1)
+        multiply(3, accs, every[3:6])
+        evacuate_one(3, accs, 1)
+        wo_turn_pass(w, grps[5], 2)
+        wo_quant(4, grps[4], both)
+
+        order = [(J, b) for J in range(3) for b in range(NB)]
+        ybanks = {}
+        for idx in range(3):
+            ybanks[idx] = turn_back(order[idx][0], order[idx][1])
+        product(4)
+        wo_quant(5, grps[5], both[0:1])
+        accs = new_accs()
+        multiply(5, accs, [(i, g) for g in range(2) for i in range(2)])
+        for idx in range(12):
+            add_residual(order[idx][0], order[idx][1], ybanks[idx])
+            if idx + 3 < 12:
+                ybanks[idx + 3] = turn_back(order[idx + 3][0], order[idx + 3][1])
+            if idx == 0:
+                wo_quant(5, grps[5], both[1:2])
+                multiply(5, accs, [(0, 2), (1, 2)])
+                evacuate(5, accs)
+
+
+        def mean(b):
+            nc.scalar.activation(out=tot[:, b, :], in_=sums[:, b, :], func=ACT.Copy, scale=-1.0 / N,
+                                 accum_out=negmu[:, b:b + 1])
+
+        def spread(b):
+            nc.scalar.activation(out=junk[:], in_=fy[b][:], func=ACT.Square, bias=negmu[:, b:b + 1], scale=1.0,
+                                 accum_out=ssq[:, b:b + 1])
+            nc.scalar.activation(out=rstd[:, b:b + 1], in_=ssq[:, b:b + 1], func=ACT.Abs_reciprocal_sqrt, bias=LN_EPS,
+                                 scale=1.0 / N)
+
+        def centre(b):
+            nc.vector.scalar_tensor_tensor(out=zt[b][:], in0=fy[b][:], scalar=negmu[:, b:b + 1], in1=g_bc[:],
+                                           op0=ALU.add, op1=ALU.mult)
+
+        def finish(b):
+            edges = [0, 640, 1280, N] if b == NB - 1 else [0, N]
+            for c in range(len(edges) - 1):
+                cols = slice(edges[c], edges[c + 1])
+                nc.vector.scalar_tensor_tensor(out=zt[b][:, cols], in0=zt[b][:, cols], scalar=rstd[:, b:b + 1],
+                                               in1=b_bc[:, cols], op0=ALU.mult, op1=ALU.add)
+                queue = nc.scalar if (b == NB - 1 and c == 1) else nc.sync
+                queue.dma_start(out=out[b, :, cols], in_=zt[b][:, cols])
+
+        for b in range(NB):
+            mean(b)
+        for b in range(NB):
+            spread(b)
+        centre(0)
+        centre(1)
+        centre(2)
+        finish(0)
+        centre(3)
+        finish(1)
+        finish(2)
+        finish(3)

@@ -36,10 +36,11 @@ def tile_hierarchicalattention_pb_kernel(tc, ctx_heads, Wo_bytes, Wo_scale, bo, 
 
         ident = const.tile([P, P], F32, name="ident")
         warm = const.tile([P, 1], F32, name="warm")
-        ones = const.tile([P, 256], F32, name="ones")
+        ident_bf = const.tile([P, P], BF16, name="ident_bf")
         scale_part = [const.tile([P, 512], F32, name="scale_part%d" % g) for g in range(PASSES)]
         scale_bc = const.tile([P, K], F32, name="scale_bc")
         bo_col = const.tile([P, 12], BF16, name="bo_col")
+        bo_f32 = const.tile([P, 4], F32, name="bo_f32")
         g_bc = const.tile([P, N], BF16, name="g_bc")
         b_bc = const.tile([P, N], BF16, name="b_bc")
         wo_raw = [const.tile([P, K], U8, name="wo_raw%d" % j) for j in range(12)]
@@ -51,13 +52,15 @@ def tile_hierarchicalattention_pb_kernel(tc, ctx_heads, Wo_bytes, Wo_scale, bo, 
                     for q in range(6)]
         wo_sc = [[const.tile([P, 256 * w], U8, name="wo_sc%d_%d" % (q, w), align_bytes=64) for w in (2, 1)]
                  for q in range(6)]
-        a_t = [const.tile([P, 512], F32, name="a_t%d" % j) for j in range(12)]
-        feat = [const.tile([P, N], BF16, name="feat%d" % b) for b in range(NB)]
+        a_t = [const.tile([P, 512], F32, name="a_t%d" % j) for j in range(8)]
+        feat = [const.tile([P, 1024], BF16, name="feat%d" % b) for b in range(NB)]
+        feat_last = const.tile([P, NB, 512], BF16, name="feat_last")
+        fb = [const.tile([P, 512], F32, name="fb%d" % b) for b in range(NB)]
         fy = [const.tile([P, N], F32, name="fy%d" % b) for b in range(NB)]
         zt = [const.tile([P, N], F32, name="zt%d" % b) for b in range(NB)]
         junk = const.tile([P, N], BF16, name="junk")
-        sums = const.tile([P, NB, 3], F32, name="sums")
-        tot = const.tile([P, NB, 3], F32, name="tot")
+        sums = const.tile([P, NB, 4], F32, name="sums")
+        tot = const.tile([P, NB, 4], F32, name="tot")
         negmu = const.tile([P, NB], F32, name="negmu")
         ssq = const.tile([P, NB], F32, name="ssq")
         rstd = const.tile([P, NB], F32, name="rstd")
@@ -80,20 +83,21 @@ def tile_hierarchicalattention_pb_kernel(tc, ctx_heads, Wo_bytes, Wo_scale, bo, 
         for j in range(1, 4):
             load_wo(j)
         load_ctx(0)
-        for j in range(4, 7):
+        for j in range(4, 6):
             load_wo(j)
+        nc.sync.dma_start(out=feat_last[:], in_=features[:, :, 1024:N].rearrange("b s f -> s b f"))
         load_ctx(1)
-        for j in range(7, 12):
+        for j in range(6, 12):
             load_wo(j)
         for b in range(NB):
-            nc.sync.dma_start(out=feat[b][:], in_=features[b])
+            nc.sync.dma_start(out=feat[b][:], in_=features[b][:, 0:1024])
         nc.sync.dma_start(out=g_bc[:], in_=ln_g.partition_broadcast(P))
         nc.sync.dma_start(out=b_bc[:], in_=ln_b.partition_broadcast(P))
         make_identity(nc, ident[:])
+        make_identity(nc, ident_bf[:])
         with nc.allow_non_contiguous_dma(reason="one bias value to a partition"):
             nc.gpsimd.dma_start(out=bo_col[:], in_=bo.rearrange("(j p) -> p j", p=P))
         nc.vector.memset(warm[:], 1.0)
-        nc.vector.memset(ones[:], 1.0)
         nc.scalar.activation(out=warm[:], in_=warm[:], func=ACT.Abs_reciprocal_sqrt)
 
         def keep_busy(words):
@@ -177,17 +181,45 @@ def tile_hierarchicalattention_pb_kernel(tc, ctx_heads, Wo_bytes, Wo_scale, bo, 
             for i in range(2):
                 evacuate_one(q, accs, i)
 
-        def turn_back(J, b):
-            ybank = y_pool.tile([P, 512], F32, name="yps", tag="yps")
-            for i in range(4):
-                nc.tensor.transpose(out=ybank[:, P * i:P * (i + 1)], in_=a_t[4 * J + i][:, P * b:P * (b + 1)],
-                                    identity=ident[:])
-            return ybank
+        def add_transposed(bank, cols, in_, last):
+            nc.tensor.matmul(out=bank[:, cols], lhsT=in_, rhs=ident[:], is_transpose=True, start=False, stop=last)
 
-        def add_residual(J, b, ybank):
-            cols = slice(512 * J, 512 * (J + 1))
-            nc.vector.scalar_tensor_tensor(out=fy[b][:, cols], in0=ybank[:], scalar=1.0, in1=feat[b][:, cols],
-                                           op0=ALU.mult, op1=ALU.add, accum_out=sums[:, b, J:J + 1])
+        def y_bank(J, b):
+            ybank = y_pool.tile([P, 512], F32, name="yps", tag="yps")
+            nc.tensor.matmul(out=ybank[:], lhsT=ident_bf[:], rhs=feat[b][:, 512 * J:512 * (J + 1)], start=True, stop=False)
+            for i in range(4):
+                add_transposed(ybank, slice(P * i, P * (i + 1)), a_t[4 * J + i][:, P * b:P * (b + 1)], i == 3)
+            nc.scalar.activation(out=fy[b][:, 512 * J:512 * (J + 1)], in_=ybank[:], func=ACT.Copy,
+                                 accum_out=sums[:, b, J:J + 1])
+
+        def fb_bank(b):
+            bank = y_pool.tile([P, 512], F32, name="yps", tag="yps")
+            nc.tensor.matmul(out=bank[:], lhsT=ident_bf[:], rhs=feat_last[:, b, :], start=True, stop=False)
+            for i in range(4):
+                add_transposed(bank, slice(P * i, P * (i + 1)), bo_f32[:, i:i + 1].to_broadcast([P, P]), i == 3)
+            nc.scalar.copy(out=fb[b][:], in_=bank[:])
+
+        def product_tokens(q, pool, tag):
+            banks = []
+            for half in range(2):
+                bank = pool.tile([P, 512], F32, name=tag, tag=tag)
+                banks.append(bank)
+                for b in (2 * half, 2 * half + 1):
+                    for g in range(PASSES):
+                        toks = slice(512 * g + P * b, 512 * g + P * (b + 1))
+                        rows = slice(256 * (g % 2), 256 * (g % 2 + 1))
+                        nc.tensor.matmul_mx(out=bank[:, 256 * (b % 2):256 * (b % 2 + 1)],
+                                            lhsT=ctx_codes[:, toks].bitcast(FP8X4), lhsT_scale=ctx_sc[:, toks],
+                                            rhs=wo_codes[q][g // 2][:, rows].bitcast(FP8X4),
+                                            rhs_scale=wo_sc[q][g // 2][:, rows],
+                                            start=(g == 0), stop=(g == PASSES - 1))
+            return banks
+
+        def add_tokens(q, b, banks):
+            nc.vector.scalar_tensor_tensor(out=fy[b][:, 256 * q:256 * (q + 1)],
+                                           in0=banks[b // 2][:, 256 * (b % 2):256 * (b % 2 + 1)], scalar=1.0,
+                                           in1=fb[b][:, 256 * (q - 4):256 * (q - 3)],
+                                           op0=ALU.mult, op1=ALU.add, accum_out=sums[:, b, q - 2:q - 1])
 
         every = [(i, g) for i in range(2) for g in range(PASSES)]
         both = [0, 1]
@@ -201,8 +233,6 @@ def tile_hierarchicalattention_pb_kernel(tc, ctx_heads, Wo_bytes, Wo_scale, bo, 
         def words_of(tile_ap, g):
             return tile_ap.bitcast(F32)[:, 256 * g:256 * (g + 1)]
 
-        for n in range(3):
-            keep_busy(ones[:])
         w = new_pair()
         widen(0, w, [(0, 0), (0, 1), (1, 0), (1, 1), (0, 2), (1, 2)])
         for g in range(PASSES):
@@ -210,19 +240,20 @@ def tile_hierarchicalattention_pb_kernel(tc, ctx_heads, Wo_bytes, Wo_scale, bo, 
         grps[0] = new_grp()
         for g in range(PASSES):
             wo_turn_pass(w, grps[0], g)
-            keep_busy(words_of(w[1], g))
+            if g == 0:
+                keep_busy(words_of(w[1], 0))
         w = new_pair()
         widen(1, w, [(0, None)])
         keep_busy(words_of(w[0], 0))
         widen(1, w, [(1, None)])
         ctx_turn(0)
-        keep_busy(words_of(w[1], 0))
         grps[1] = wo_turn(w)
         wo_quant(0, grps[0], both)
         w = new_pair()
-        widen(2, w, [(0, None)])
-        keep_busy(words_of(w[0], 0))
-        widen(2, w, [(1, None)])
+        widen(2, w, [(0, None), (1, None)])
+        nc.scalar.copy(out=bo_f32[:], in_=bo_col[:, 8:12])
+        for b in range(NB):
+            fb_bank(b)
         grps[2] = wo_turn(w)
         keep_busy(words_of(w[1], 0))
         wo_quant(1, grps[1], both)
@@ -236,40 +267,28 @@ def tile_hierarchicalattention_pb_kernel(tc, ctx_heads, Wo_bytes, Wo_scale, bo, 
         wo_quant(2, grps[2], both)
         product(0)
         product(1)
-        product(2)
         w = new_pair()
         widen(4, w, [(0, None), (1, None)])
         grps[4] = wo_turn(w)
+        product(2)
         wo_quant(3, grps[3], both)
-        accs = new_accs()
-        multiply(3, accs, every[0:3])
-        evacuate_one(3, accs, 0)
         w = new_pair()
         widen(5, w, [(i, g) for g in range(PASSES) for i in range(2)])
         grps[5] = new_grp()
         wo_turn_pass(w, grps[5], 0)
         wo_turn_pass(w, grps[5], 1)
-        multiply(3, accs, every[3:6])
-        evacuate_one(3, accs, 1)
+        product(3)
         wo_turn_pass(w, grps[5], 2)
         wo_quant(4, grps[4], both)
-
-        order = [(J, b) for J in range(3) for b in range(NB)]
-        ybanks = {}
-        for idx in range(3):
-            ybanks[idx] = turn_back(order[idx][0], order[idx][1])
-        product(4)
-        wo_quant(5, grps[5], both[0:1])
-        accs = new_accs()
-        multiply(5, accs, [(i, g) for g in range(2) for i in range(2)])
-        for idx in range(12):
-            add_residual(order[idx][0], order[idx][1], ybanks[idx])
-            if idx + 3 < 12:
-                ybanks[idx + 3] = turn_back(order[idx + 3][0], order[idx + 3][1])
-            if idx == 0:
-                wo_quant(5, grps[5], both[1:2])
-                multiply(5, accs, [(0, 2), (1, 2)])
-                evacuate(5, accs)
+        banks4 = product_tokens(4, acc_pool, "acc")
+        y_bank(0, 0)
+        y_bank(1, 0)
+        wo_quant(5, grps[5], both)
+        banks5 = product_tokens(5, tp_pool, "tp")
+        for b in range(NB):
+            add_tokens(4, b, banks4)
+        for b in range(NB):
+            add_tokens(5, b, banks5)
 
 
         def mean(b):
@@ -295,10 +314,20 @@ def tile_hierarchicalattention_pb_kernel(tc, ctx_heads, Wo_bytes, Wo_scale, bo, 
                 queue = nc.scalar if (b == NB - 1 and c == 1) else nc.sync
                 queue.dma_start(out=out[b, :, cols], in_=zt[b][:, cols])
 
-        for b in range(NB):
-            mean(b)
-        for b in range(NB):
-            spread(b)
+        mean(0)
+        y_bank(0, 1)
+        y_bank(1, 1)
+        mean(1)
+        y_bank(0, 2)
+        y_bank(1, 2)
+        mean(2)
+        spread(0)
+        y_bank(0, 3)
+        y_bank(1, 3)
+        mean(3)
+        spread(1)
+        spread(2)
+        spread(3)
         centre(0)
         centre(1)
         centre(2)

@@ -37,7 +37,8 @@ def tile_hierarchicalattention_pb_kernel(tc, ctx_heads, Wo_bytes, Wo_scale, bo, 
         ident = const.tile([P, P], F32, name="ident")
         warm = const.tile([P, 1], F32, name="warm")
         ident_bf = const.tile([P, P], BF16, name="ident_bf")
-        scale_part = [const.tile([P, 512], F32, name="scale_part%d" % g) for g in range(PASSES)]
+        scale_rows = const.tile([P, P], F32, name="scale_rows")
+        scale_col = const.tile([P, 12], F32, name="scale_col")
         scale_bc = const.tile([P, K], F32, name="scale_bc")
         bo_col = const.tile([P, 12], BF16, name="bo_col")
         bo_f32 = const.tile([P, 4], F32, name="bo_f32")
@@ -65,10 +66,6 @@ def tile_hierarchicalattention_pb_kernel(tc, ctx_heads, Wo_bytes, Wo_scale, bo, 
         ssq = const.tile([P, NB], F32, name="ssq")
         rstd = const.tile([P, NB], F32, name="rstd")
 
-        scale_row = Wo_scale.rearrange("o k -> (o k)")
-        def load_scale(queue, g):
-            queue.dma_start(out=scale_part[g][:], in_=scale_row[512 * g:512 * (g + 1)].partition_broadcast(P))
-
         def load_wo(j):
             nc.sync.dma_start(out=wo_raw[j][:], in_=Wo_bytes[P * j:P * (j + 1), :])
 
@@ -76,18 +73,19 @@ def tile_hierarchicalattention_pb_kernel(tc, ctx_heads, Wo_bytes, Wo_scale, bo, 
             nc.sync.dma_start(out=ctx_sb[bp][:].rearrange("p b (h d) -> p (b h) d", h=12),
                               in_=ctx_heads[2 * bp:2 * bp + 2].rearrange("b h s d -> s (b h) d"))
 
-        load_scale(nc.scalar, 0)
-        load_scale(nc.scalar, 2)
+        nc.gpsimd.memset(scale_rows[:], 0.0)
+        nc.sync.dma_start(out=scale_rows[0:12, :], in_=Wo_scale.rearrange("o (j p) -> (o j) p", p=P))
         load_wo(0)
-        load_scale(nc.sync, 1)
         for j in range(1, 4):
             load_wo(j)
         load_ctx(0)
-        for j in range(4, 6):
+        for j in range(4, 7):
+            load_wo(j)
+        load_ctx(1)
+        for j in range(7, 9):
             load_wo(j)
         nc.sync.dma_start(out=feat_last[:], in_=features[:, :, 1024:N].rearrange("b s f -> s b f"))
-        load_ctx(1)
-        for j in range(6, 12):
+        for j in range(9, 12):
             load_wo(j)
         for b in range(NB):
             nc.sync.dma_start(out=feat[b][:], in_=features[b][:, 0:1024])
@@ -112,7 +110,7 @@ def tile_hierarchicalattention_pb_kernel(tc, ctx_heads, Wo_bytes, Wo_scale, bo, 
             for i, g in pieces:
                 cols = slice(0, K) if g is None else slice(512 * g, 512 * (g + 1))
                 nc.vector.tensor_tensor(out=two[i][:, cols], in0=wo_raw[2 * q + i][:, cols].bitcast(FP8),
-                                        in1=(scale_part[g][:] if q == 0 else scale_bc[:, cols]), op=ALU.mult)
+                                        in1=scale_bc[:, cols], op=ALU.mult)
 
         def turn_bank(two, g):
             bank = tp_pool.tile([P, 2, 2, P], F32, name="tp", tag="tp")
@@ -233,10 +231,17 @@ def tile_hierarchicalattention_pb_kernel(tc, ctx_heads, Wo_bytes, Wo_scale, bo, 
         def words_of(tile_ap, g):
             return tile_ap.bitcast(F32)[:, 256 * g:256 * (g + 1)]
 
-        w = new_pair()
-        widen(0, w, [(0, 0), (0, 1), (1, 0), (1, 1), (0, 2), (1, 2)])
+        turned = y_pool.tile([P, 512], F32, name="yps", tag="yps")
+        nc.tensor.transpose(out=turned[:, 0:P], in_=scale_rows[:], identity=ident[:])
+        nc.scalar.copy(out=scale_col[:], in_=turned[:, 0:12])
         for g in range(PASSES):
-            nc.scalar.copy(out=scale_bc[:, 512 * g:512 * (g + 1)], in_=scale_part[g][:])
+            spread_bank = y_pool.tile([P, 512], F32, name="yps", tag="yps")
+            for i in range(4):
+                nc.tensor.transpose(out=spread_bank[:, P * i:P * (i + 1)],
+                                    in_=scale_col[:, 4 * g + i:4 * g + i + 1].to_broadcast([P, P]), identity=ident[:])
+            nc.scalar.copy(out=scale_bc[:, 512 * g:512 * (g + 1)], in_=spread_bank[:])
+        w = new_pair()
+        widen(0, w, [(i, g) for g in range(PASSES) for i in range(2)])
         grps[0] = new_grp()
         for g in range(PASSES):
             wo_turn_pass(w, grps[0], g)
@@ -251,9 +256,6 @@ def tile_hierarchicalattention_pb_kernel(tc, ctx_heads, Wo_bytes, Wo_scale, bo, 
         wo_quant(0, grps[0], both)
         w = new_pair()
         widen(2, w, [(0, None), (1, None)])
-        nc.scalar.copy(out=bo_f32[:], in_=bo_col[:, 8:12])
-        for b in range(NB):
-            fb_bank(b)
         grps[2] = wo_turn(w)
         keep_busy(words_of(w[1], 0))
         wo_quant(1, grps[1], both)
@@ -262,7 +264,12 @@ def tile_hierarchicalattention_pb_kernel(tc, ctx_heads, Wo_bytes, Wo_scale, bo, 
         widen(3, w, [(0, None)])
         keep_busy(words_of(w[0], 0))
         widen(3, w, [(1, None)])
+        nc.scalar.copy(out=bo_f32[:], in_=bo_col[:, 8:12])
+        fb_bank(0)
+        fb_bank(1)
         grps[3] = wo_turn(w)
+        fb_bank(2)
+        fb_bank(3)
         ctx_quant()
         wo_quant(2, grps[2], both)
         product(0)

@@ -37,7 +37,6 @@ def tile_hierarchicalattention_pb_kernel(tc, ctx_heads, Wo_bytes, Wo_scale, bo, 
         ident = const.tile([P, P], F32, name="ident")
         warm = const.tile([P, 1], F32, name="warm")
         ident_bf = const.tile([P, P], BF16, name="ident_bf")
-        scale_rows = const.tile([P, P], F32, name="scale_rows")
         scale_col = const.tile([P, 12], F32, name="scale_col")
         scale_bc = const.tile([P, K], F32, name="scale_bc")
         bo_col = const.tile([P, 12], BF16, name="bo_col")
@@ -73,22 +72,23 @@ def tile_hierarchicalattention_pb_kernel(tc, ctx_heads, Wo_bytes, Wo_scale, bo, 
             nc.sync.dma_start(out=ctx_sb[bp][:].rearrange("p b (h d) -> p (b h) d", h=12),
                               in_=ctx_heads[2 * bp:2 * bp + 2].rearrange("b h s d -> s (b h) d"))
 
-        nc.gpsimd.memset(scale_rows[:], 0.0)
-        nc.sync.dma_start(out=scale_rows[0:12, :], in_=Wo_scale.rearrange("o (j p) -> (o j) p", p=P))
+        with nc.allow_non_contiguous_dma(reason="four scales in a row to a partition, three times"):
+            nc.sync.dma_start(out=scale_col[:].rearrange("p (g t) -> p g t", t=4),
+                              in_=Wo_scale.rearrange("o (g p t) -> p (o g) t", p=P, t=4))
         load_wo(0)
-        for j in range(1, 4):
-            load_wo(j)
+        load_wo(1)
         load_ctx(0)
-        for j in range(4, 7):
+        for j in range(2, 5):
             load_wo(j)
         load_ctx(1)
-        for j in range(7, 9):
-            load_wo(j)
+        load_wo(5)
         nc.sync.dma_start(out=feat_last[:], in_=features[:, :, 1024:N].rearrange("b s f -> s b f"))
-        for j in range(9, 12):
+        for j in range(6, 8):
             load_wo(j)
         for b in range(NB):
             nc.sync.dma_start(out=feat[b][:], in_=features[b][:, 0:1024])
+        for j in range(8, 12):
+            load_wo(j)
         nc.sync.dma_start(out=g_bc[:], in_=ln_g.partition_broadcast(P))
         nc.sync.dma_start(out=b_bc[:], in_=ln_b.partition_broadcast(P))
         make_identity(nc, ident[:])
@@ -231,67 +231,65 @@ def tile_hierarchicalattention_pb_kernel(tc, ctx_heads, Wo_bytes, Wo_scale, bo, 
         def words_of(tile_ap, g):
             return tile_ap.bitcast(F32)[:, 256 * g:256 * (g + 1)]
 
-        turned = y_pool.tile([P, 512], F32, name="yps", tag="yps")
-        nc.tensor.transpose(out=turned[:, 0:P], in_=scale_rows[:], identity=ident[:])
-        nc.scalar.copy(out=scale_col[:], in_=turned[:, 0:12])
         for g in range(PASSES):
-            spread_bank = y_pool.tile([P, 512], F32, name="yps", tag="yps")
-            for i in range(4):
-                nc.tensor.transpose(out=spread_bank[:, P * i:P * (i + 1)],
-                                    in_=scale_col[:, 4 * g + i:4 * g + i + 1].to_broadcast([P, P]), identity=ident[:])
-            nc.scalar.copy(out=scale_bc[:, 512 * g:512 * (g + 1)], in_=spread_bank[:])
+            spread_bank = y_pool.tile([P, 4, P], F32, name="yps", tag="yps")
+            for t in range(4):
+                nc.tensor.transpose(out=spread_bank[:, t, :],
+                                    in_=scale_col[:, 4 * g + t:4 * g + t + 1].to_broadcast([P, P]), identity=ident[:])
+            nc.scalar.copy(out=scale_bc[:, 512 * g:512 * (g + 1)].rearrange("m (p t) -> m p t", t=4),
+                           in_=spread_bank[:].rearrange("m t p -> m p t"))
         w = new_pair()
         widen(0, w, [(i, g) for g in range(PASSES) for i in range(2)])
         grps[0] = new_grp()
         for g in range(PASSES):
             wo_turn_pass(w, grps[0], g)
-            if g == 0:
-                keep_busy(words_of(w[1], 0))
+            if g != 1:
+                keep_busy(words_of(w[1], g))
+        ctx_turn(0)
         w = new_pair()
         widen(1, w, [(0, None)])
         keep_busy(words_of(w[0], 0))
         widen(1, w, [(1, None)])
-        ctx_turn(0)
         grps[1] = wo_turn(w)
+        keep_busy(words_of(w[1], 0))
+        ctx_turn(1)
         wo_quant(0, grps[0], both)
         w = new_pair()
         widen(2, w, [(0, None), (1, None)])
-        grps[2] = wo_turn(w)
-        keep_busy(words_of(w[1], 0))
-        wo_quant(1, grps[1], both)
-        ctx_turn(1)
-        w = new_pair()
-        widen(3, w, [(0, None)])
-        keep_busy(words_of(w[0], 0))
-        widen(3, w, [(1, None)])
         nc.scalar.copy(out=bo_f32[:], in_=bo_col[:, 8:12])
-        fb_bank(0)
-        fb_bank(1)
-        grps[3] = wo_turn(w)
-        fb_bank(2)
-        fb_bank(3)
+        for b in range(NB):
+            fb_bank(b)
+        grps[2] = wo_turn(w)
+        wo_quant(1, grps[1], both)
         ctx_quant()
-        wo_quant(2, grps[2], both)
         product(0)
         product(1)
         w = new_pair()
+        widen(3, w, [(0, None), (1, None)])
+        grps[3] = wo_turn(w)
+        wo_quant(2, grps[2], both)
+        product(2)
+        y_bank(0, 0)
+        y_bank(0, 1)
+        w = new_pair()
         widen(4, w, [(0, None), (1, None)])
         grps[4] = wo_turn(w)
-        product(2)
+        y_bank(0, 2)
+        y_bank(0, 3)
         wo_quant(3, grps[3], both)
         w = new_pair()
         widen(5, w, [(i, g) for g in range(PASSES) for i in range(2)])
         grps[5] = new_grp()
         wo_turn_pass(w, grps[5], 0)
-        wo_turn_pass(w, grps[5], 1)
         product(3)
+        wo_turn_pass(w, grps[5], 1)
         wo_turn_pass(w, grps[5], 2)
         wo_quant(4, grps[4], both)
         banks4 = product_tokens(4, acc_pool, "acc")
-        y_bank(0, 0)
         y_bank(1, 0)
         wo_quant(5, grps[5], both)
         banks5 = product_tokens(5, tp_pool, "tp")
+        y_bank(1, 1)
         for b in range(NB):
             add_tokens(4, b, banks4)
         for b in range(NB):
@@ -322,14 +320,10 @@ def tile_hierarchicalattention_pb_kernel(tc, ctx_heads, Wo_bytes, Wo_scale, bo, 
                 queue.dma_start(out=out[b, :, cols], in_=zt[b][:, cols])
 
         mean(0)
-        y_bank(0, 1)
-        y_bank(1, 1)
         mean(1)
-        y_bank(0, 2)
         y_bank(1, 2)
         mean(2)
         spread(0)
-        y_bank(0, 3)
         y_bank(1, 3)
         mean(3)
         spread(1)

@@ -98,10 +98,6 @@ def tile_hierarchicalattention_pb_kernel(tc, ctx_heads, Wo_bytes, Wo_scale, bo, 
         nc.vector.memset(warm[:], 1.0)
         nc.scalar.activation(out=warm[:], in_=warm[:], func=ACT.Abs_reciprocal_sqrt)
 
-        def keep_busy(words):
-            scratch = y_pool.tile([P, 512], F32, name="yps", tag="yps")
-            nc.tensor.matmul(out=scratch[:, 0:256], lhsT=ident[:], rhs=words, start=True, stop=True)
-
         def new_pair():
             two = [wbf_pool.tile([P, K], BF16, name="wbf", tag="wbf") for i in range(2)]
             return [two[0][:], two[1][:]]
@@ -228,9 +224,6 @@ def tile_hierarchicalattention_pb_kernel(tc, ctx_heads, Wo_bytes, Wo_scale, bo, 
             multiply(q, accs, every)
             evacuate(q, accs)
 
-        def words_of(tile_ap, g):
-            return tile_ap.bitcast(F32)[:, 256 * g:256 * (g + 1)]
-
         for g in range(PASSES):
             spread_bank = y_pool.tile([P, 4, P], F32, name="yps", tag="yps")
             for t in range(4):
@@ -240,26 +233,21 @@ def tile_hierarchicalattention_pb_kernel(tc, ctx_heads, Wo_bytes, Wo_scale, bo, 
                            in_=spread_bank[:].rearrange("m t p -> m p t"))
         w = new_pair()
         widen(0, w, [(i, g) for g in range(PASSES) for i in range(2)])
-        grps[0] = new_grp()
-        for g in range(PASSES):
-            wo_turn_pass(w, grps[0], g)
-            if g != 1:
-                keep_busy(words_of(w[1], g))
+        grps[0] = wo_turn(w)
         ctx_turn(0)
         w = new_pair()
-        widen(1, w, [(0, None)])
-        keep_busy(words_of(w[0], 0))
-        widen(1, w, [(1, None)])
+        widen(1, w, [(0, None), (1, None)])
         grps[1] = wo_turn(w)
-        keep_busy(words_of(w[1], 0))
         ctx_turn(1)
         wo_quant(0, grps[0], both)
         w = new_pair()
         widen(2, w, [(0, None), (1, None)])
         nc.scalar.copy(out=bo_f32[:], in_=bo_col[:, 8:12])
-        for b in range(NB):
-            fb_bank(b)
+        fb_bank(0)
+        fb_bank(1)
         grps[2] = wo_turn(w)
+        fb_bank(2)
+        fb_bank(3)
         wo_quant(1, grps[1], both)
         ctx_quant()
         product(0)
@@ -274,22 +262,16 @@ def tile_hierarchicalattention_pb_kernel(tc, ctx_heads, Wo_bytes, Wo_scale, bo, 
         w = new_pair()
         widen(4, w, [(0, None), (1, None)])
         grps[4] = wo_turn(w)
-        y_bank(0, 2)
-        y_bank(0, 3)
         wo_quant(3, grps[3], both)
+        product(3)
         w = new_pair()
         widen(5, w, [(i, g) for g in range(PASSES) for i in range(2)])
-        grps[5] = new_grp()
-        wo_turn_pass(w, grps[5], 0)
-        product(3)
-        wo_turn_pass(w, grps[5], 1)
-        wo_turn_pass(w, grps[5], 2)
+        grps[5] = wo_turn(w)
+        y_bank(1, 0)
         wo_quant(4, grps[4], both)
         banks4 = product_tokens(4, acc_pool, "acc")
-        y_bank(1, 0)
         wo_quant(5, grps[5], both)
         banks5 = product_tokens(5, tp_pool, "tp")
-        y_bank(1, 1)
         for b in range(NB):
             add_tokens(4, b, banks4)
         for b in range(NB):
@@ -320,10 +302,13 @@ def tile_hierarchicalattention_pb_kernel(tc, ctx_heads, Wo_bytes, Wo_scale, bo, 
                 queue.dma_start(out=out[b, :, cols], in_=zt[b][:, cols])
 
         mean(0)
+        y_bank(1, 1)
         mean(1)
+        y_bank(0, 2)
         y_bank(1, 2)
         mean(2)
         spread(0)
+        y_bank(0, 3)
         y_bank(1, 3)
         mean(3)
         spread(1)

@@ -41,6 +41,7 @@ def tile_hierarchicalattention_pb_kernel(tc, ctx_heads, Wo_bytes, Wo_scale, bo, 
         scale_bc = const.tile([P, K], F32, name="scale_bc")
         bo_col = const.tile([P, 12], BF16, name="bo_col")
         bo_f32 = const.tile([P, 4], F32, name="bo_f32")
+        bo_bc = const.tile([P, 512], F32, name="bo_bc")
         g_bc = const.tile([P, N], BF16, name="g_bc")
         b_bc = const.tile([P, N], BF16, name="b_bc")
         wo_raw = [const.tile([P, K], U8, name="wo_raw%d" % j) for j in range(12)]
@@ -186,12 +187,16 @@ def tile_hierarchicalattention_pb_kernel(tc, ctx_heads, Wo_bytes, Wo_scale, bo, 
             nc.scalar.activation(out=fy[b][:, 512 * J:512 * (J + 1)], in_=ybank[:], func=ACT.Copy,
                                  accum_out=sums[:, b, J:J + 1])
 
-        def fb_bank(b):
+        def spread_bo():
+            nc.scalar.copy(out=bo_f32[:], in_=bo_col[:, 8:12])
             bank = y_pool.tile([P, 512], F32, name="yps", tag="yps")
-            nc.tensor.matmul(out=bank[:], lhsT=ident_bf[:], rhs=feat_last[:, b, :], start=True, stop=False)
             for i in range(4):
-                add_transposed(bank, slice(P * i, P * (i + 1)), bo_f32[:, i:i + 1].to_broadcast([P, P]), i == 3)
-            nc.scalar.copy(out=fb[b][:], in_=bank[:])
+                nc.tensor.transpose(out=bank[:, P * i:P * (i + 1)], in_=bo_f32[:, i:i + 1].to_broadcast([P, P]),
+                                    identity=ident[:])
+            nc.scalar.copy(out=bo_bc[:], in_=bank[:])
+
+        def features_and_bo(b):
+            nc.vector.tensor_tensor(out=fb[b][:], in0=feat_last[:, b, :], in1=bo_bc[:], op=ALU.add)
 
         def product_tokens(q, pool, tag):
             banks = []
@@ -242,12 +247,8 @@ def tile_hierarchicalattention_pb_kernel(tc, ctx_heads, Wo_bytes, Wo_scale, bo, 
         wo_quant(0, grps[0], both)
         w = new_pair()
         widen(2, w, [(0, None), (1, None)])
-        nc.scalar.copy(out=bo_f32[:], in_=bo_col[:, 8:12])
-        fb_bank(0)
-        fb_bank(1)
         grps[2] = wo_turn(w)
-        fb_bank(2)
-        fb_bank(3)
+        spread_bo()
         wo_quant(1, grps[1], both)
         ctx_quant()
         product(0)
@@ -256,6 +257,8 @@ def tile_hierarchicalattention_pb_kernel(tc, ctx_heads, Wo_bytes, Wo_scale, bo, 
         widen(3, w, [(0, None), (1, None)])
         grps[3] = wo_turn(w)
         wo_quant(2, grps[2], both)
+        features_and_bo(0)
+        features_and_bo(1)
         product(2)
         y_bank(0, 0)
         y_bank(0, 1)
@@ -263,6 +266,8 @@ def tile_hierarchicalattention_pb_kernel(tc, ctx_heads, Wo_bytes, Wo_scale, bo, 
         widen(4, w, [(0, None), (1, None)])
         grps[4] = wo_turn(w)
         wo_quant(3, grps[3], both)
+        features_and_bo(2)
+        features_and_bo(3)
         product(3)
         w = new_pair()
         widen(5, w, [(i, g) for g in range(PASSES) for i in range(2)])

@@ -257,8 +257,6 @@ def tile_hierarchicalattention_pb_kernel(tc, ctx_heads, Wo_bytes, Wo_scale, bo, 
         widen(3, w, [(0, None), (1, None)])
         grps[3] = wo_turn(w)
         wo_quant(2, grps[2], both)
-        features_and_bo(0)
-        features_and_bo(1)
         product(2)
         y_bank(0, 0)
         y_bank(0, 1)
@@ -266,15 +264,17 @@ def tile_hierarchicalattention_pb_kernel(tc, ctx_heads, Wo_bytes, Wo_scale, bo, 
         widen(4, w, [(0, None), (1, None)])
         grps[4] = wo_turn(w)
         wo_quant(3, grps[3], both)
-        features_and_bo(2)
-        features_and_bo(3)
         product(3)
         w = new_pair()
         widen(5, w, [(i, g) for g in range(PASSES) for i in range(2)])
         grps[5] = wo_turn(w)
         y_bank(1, 0)
+        features_and_bo(0)
+        features_and_bo(1)
         wo_quant(4, grps[4], both)
         banks4 = product_tokens(4, acc_pool, "acc")
+        features_and_bo(2)
+        features_and_bo(3)
         wo_quant(5, grps[5], both)
         banks5 = product_tokens(5, tp_pool, "tp")
         for b in range(NB):

@@ -99,6 +99,10 @@ def tile_hierarchicalattention_pb_kernel(tc, ctx_heads, Wo_bytes, Wo_scale, bo, 
         nc.vector.memset(warm[:], 1.0)
         nc.scalar.activation(out=warm[:], in_=warm[:], func=ACT.Abs_reciprocal_sqrt)
 
+        def keep_busy():
+            scratch = y_pool.tile([P, 512], F32, name="yps", tag="yps")
+            nc.tensor.matmul(out=scratch[:, 0:256], lhsT=ident[:], rhs=scale_bc[:, 0:256], start=True, stop=True)
+
         def new_pair():
             two = [wbf_pool.tile([P, K], BF16, name="wbf", tag="wbf") for i in range(2)]
             return [two[0][:], two[1][:]]
@@ -239,15 +243,20 @@ def tile_hierarchicalattention_pb_kernel(tc, ctx_heads, Wo_bytes, Wo_scale, bo, 
         w = new_pair()
         widen(0, w, [(i, g) for g in range(PASSES) for i in range(2)])
         grps[0] = wo_turn(w)
+        keep_busy()
         ctx_turn(0)
         w = new_pair()
         widen(1, w, [(0, None), (1, None)])
+        keep_busy()
         grps[1] = wo_turn(w)
+        keep_busy()
         ctx_turn(1)
         wo_quant(0, grps[0], both)
         w = new_pair()
         widen(2, w, [(0, None), (1, None)])
+        keep_busy()
         grps[2] = wo_turn(w)
+        keep_busy()
         spread_bo()
         wo_quant(1, grps[1], both)
         ctx_quant()

@@ -39,8 +39,8 @@ def tile_hierarchicalattention_pb_kernel(tc, ctx_heads, Wo_bytes, Wo_scale, bo, 
         ident_bf = const.tile([P, P], BF16, name="ident_bf")
         scale_col = const.tile([P, 12], F32, name="scale_col")
         scale_bc = const.tile([P, K], F32, name="scale_bc")
-        bo_col = const.tile([P, 12], BF16, name="bo_col")
-        bo_f32 = const.tile([P, 4], F32, name="bo_f32")
+        bo_rows = const.tile([P, P], BF16, name="bo_rows")
+        bo_col = const.tile([P, 12], F32, name="bo_col")
         bo_bc = const.tile([P, 512], F32, name="bo_bc")
         g_bc = const.tile([P, N], BF16, name="g_bc")
         b_bc = const.tile([P, N], BF16, name="b_bc")
@@ -73,11 +73,13 @@ def tile_hierarchicalattention_pb_kernel(tc, ctx_heads, Wo_bytes, Wo_scale, bo, 
             nc.sync.dma_start(out=ctx_sb[bp][:].rearrange("p b (h d) -> p (b h) d", h=12),
                               in_=ctx_heads[2 * bp:2 * bp + 2].rearrange("b h s d -> s (b h) d"))
 
+        nc.gpsimd.memset(bo_rows[:], 0.0)
         with nc.allow_non_contiguous_dma(reason="four scales in a row to a partition, three times"):
             nc.sync.dma_start(out=scale_col[:].rearrange("p (g t) -> p g t", t=4),
                               in_=Wo_scale.rearrange("o (g p t) -> p (o g) t", p=P, t=4))
         load_wo(0)
         load_wo(1)
+        nc.sync.dma_start(out=bo_rows[0:12, :], in_=bo.rearrange("(j p) -> j p", p=P))
         load_ctx(0)
         for j in range(2, 5):
             load_wo(j)
@@ -94,8 +96,6 @@ def tile_hierarchicalattention_pb_kernel(tc, ctx_heads, Wo_bytes, Wo_scale, bo, 
         nc.sync.dma_start(out=b_bc[:], in_=ln_b.partition_broadcast(P))
         make_identity(nc, ident[:])
         make_identity(nc, ident_bf[:])
-        with nc.allow_non_contiguous_dma(reason="one bias value to a partition"):
-            nc.gpsimd.dma_start(out=bo_col[:], in_=bo.rearrange("(j p) -> p j", p=P))
         nc.vector.memset(warm[:], 1.0)
         nc.scalar.activation(out=warm[:], in_=warm[:], func=ACT.Abs_reciprocal_sqrt)
 
@@ -192,10 +192,9 @@ def tile_hierarchicalattention_pb_kernel(tc, ctx_heads, Wo_bytes, Wo_scale, bo, 
                                  accum_out=sums[:, b, J:J + 1])
 
         def spread_bo():
-            nc.scalar.copy(out=bo_f32[:], in_=bo_col[:, 8:12])
             bank = y_pool.tile([P, 512], F32, name="yps", tag="yps")
             for i in range(4):
-                nc.tensor.transpose(out=bank[:, P * i:P * (i + 1)], in_=bo_f32[:, i:i + 1].to_broadcast([P, P]),
+                nc.tensor.transpose(out=bank[:, P * i:P * (i + 1)], in_=bo_col[:, 8 + i:9 + i].to_broadcast([P, P]),
                                     identity=ident[:])
             nc.scalar.copy(out=bo_bc[:], in_=bank[:])
 
@@ -243,6 +242,9 @@ def tile_hierarchicalattention_pb_kernel(tc, ctx_heads, Wo_bytes, Wo_scale, bo, 
         w = new_pair()
         widen(0, w, [(i, g) for g in range(PASSES) for i in range(2)])
         grps[0] = wo_turn(w)
+        bo_turned = y_pool.tile([P, P], BF16, name="yps", tag="yps")
+        nc.tensor.transpose(out=bo_turned[:], in_=bo_rows[:], identity=ident_bf[:])
+        nc.scalar.copy(out=bo_col[:], in_=bo_turned[:, 0:12])
         keep_busy()
         ctx_turn(0)
         w = new_pair()

@@ -21,6 +21,7 @@ N = 1536
 NB = 4
 PASSES = 3
 LN_EPS = 1e-5
+OWN_FROM = [768, 1024, N, N]
 
 
 def tile_hierarchicalattention_pb_kernel(tc, ctx_heads, Wo_bytes, Wo_scale, bo, features, ln_g, ln_b, out):
@@ -44,6 +45,9 @@ def tile_hierarchicalattention_pb_kernel(tc, ctx_heads, Wo_bytes, Wo_scale, bo, 
         bo_bc = const.tile([P, 512], F32, name="bo_bc")
         g_bc = const.tile([P, N], BF16, name="g_bc")
         b_bc = const.tile([P, N], BF16, name="b_bc")
+        gb_rows = const.tile([P, P], BF16, name="gb_rows")
+        gb_col = const.tile([P, 24], BF16, name="gb_col")
+        gz = [const.tile([P, N - OWN_FROM[b]], F32, name="gz%d" % b) for b in range(2)]
         wo_raw = [const.tile([P, K], U8, name="wo_raw%d" % j) for j in range(12)]
         ctx_sb = [const.tile([P, 2, K], BF16, name="ctx_sb%d" % bp) for bp in range(2)]
         cgrp = const.tile([P, PASSES * 2048], BF16, name="cgrp", align_bytes=64)
@@ -74,6 +78,7 @@ def tile_hierarchicalattention_pb_kernel(tc, ctx_heads, Wo_bytes, Wo_scale, bo, 
                               in_=ctx_heads[2 * bp:2 * bp + 2].rearrange("b h s d -> s (b h) d"))
 
         nc.gpsimd.memset(bo_rows[:], 0.0)
+        nc.gpsimd.memset(gb_rows[:], 0.0)
         with nc.allow_non_contiguous_dma(reason="four scales in a row to a partition, three times"):
             nc.sync.dma_start(out=scale_col[:].rearrange("p (g t) -> p g t", t=4),
                               in_=Wo_scale.rearrange("o (g p t) -> p (o g) t", p=P, t=4))
@@ -92,6 +97,8 @@ def tile_hierarchicalattention_pb_kernel(tc, ctx_heads, Wo_bytes, Wo_scale, bo, 
             nc.sync.dma_start(out=feat[b][:], in_=features[b][:, 0:1024])
         for j in range(8, 12):
             load_wo(j)
+        nc.sync.dma_start(out=gb_rows[0:12, :], in_=ln_g.rearrange("(j p) -> j p", p=P))
+        nc.sync.dma_start(out=gb_rows[12:24, :], in_=ln_b.rearrange("(j p) -> j p", p=P))
         nc.sync.dma_start(out=g_bc[:], in_=ln_g.partition_broadcast(P))
         nc.sync.dma_start(out=b_bc[:], in_=ln_b.partition_broadcast(P))
         make_identity(nc, ident[:])
@@ -223,6 +230,18 @@ def tile_hierarchicalattention_pb_kernel(tc, ctx_heads, Wo_bytes, Wo_scale, bo, 
                                            in1=fb[b][:, 256 * (q - 4):256 * (q - 3)],
                                            op0=ALU.mult, op1=ALU.add, accum_out=sums[:, b, q - 2:q - 1])
 
+        def turn_gain_shift():
+            turned = y_pool.tile([P, P], BF16, name="yps", tag="yps")
+            nc.tensor.transpose(out=turned[:], in_=gb_rows[:], identity=ident_bf[:])
+            nc.scalar.copy(out=gb_col[:], in_=turned[:, 0:24])
+
+        def spread_columns(pool, tag, columns):
+            bank = pool.tile([P, 1024], BF16, name=tag, tag=tag)
+            for i, j in enumerate(columns):
+                nc.tensor.transpose(out=bank[:, P * i:P * (i + 1)], in_=gb_col[:, j:j + 1].to_broadcast([P, P]),
+                                    identity=ident_bf[:])
+            return bank
+
         every = [(i, g) for i in range(2) for g in range(PASSES)]
         both = [0, 1]
         grps = {}
@@ -274,16 +293,19 @@ def tile_hierarchicalattention_pb_kernel(tc, ctx_heads, Wo_bytes, Wo_scale, bo, 
         w = new_pair()
         widen(4, w, [(0, None), (1, None)])
         grps[4] = wo_turn(w)
+        turn_gain_shift()
         wo_quant(3, grps[3], both)
         product(3)
         w = new_pair()
         widen(5, w, [(i, g) for g in range(PASSES) for i in range(2)])
         grps[5] = wo_turn(w)
         y_bank(1, 0)
+        y_bank(1, 1)
         features_and_bo(0)
         features_and_bo(1)
         wo_quant(4, grps[4], both)
         banks4 = product_tokens(4, acc_pool, "acc")
+        y_bank(0, 2)
         features_and_bo(2)
         features_and_bo(3)
         wo_quant(5, grps[5], both)
@@ -304,37 +326,64 @@ def tile_hierarchicalattention_pb_kernel(tc, ctx_heads, Wo_bytes, Wo_scale, bo, 
             nc.scalar.activation(out=rstd[:, b:b + 1], in_=ssq[:, b:b + 1], func=ACT.Abs_reciprocal_sqrt, bias=LN_EPS,
                                  scale=1.0 / N)
 
-        def centre(b):
-            nc.vector.scalar_tensor_tensor(out=zt[b][:], in0=fy[b][:], scalar=negmu[:, b:b + 1], in1=g_bc[:],
-                                           op0=ALU.add, op1=ALU.mult)
+        def pieces(lo, hi, edges):
+            cuts = [lo] + [e for e in edges if lo < e < hi] + [hi]
+            return [(cuts[i], cuts[i + 1]) for i in range(len(cuts) - 1)]
 
-        def finish(b):
-            edges = [0, 640, 1280, N] if b == NB - 1 else [0, N]
-            for c in range(len(edges) - 1):
-                cols = slice(edges[c], edges[c + 1])
-                nc.vector.scalar_tensor_tensor(out=zt[b][:, cols], in0=zt[b][:, cols], scalar=rstd[:, b:b + 1],
-                                               in1=b_bc[:, cols], op0=ALU.mult, op1=ALU.add)
-                queue = nc.scalar if (b == NB - 1 and c == 1) else nc.sync
-                queue.dma_start(out=out[b, :, cols], in_=zt[b][:, cols])
+        def centre(b, gain):
+            for lo, hi in pieces(0, OWN_FROM[b], [1024]):
+                nc.vector.scalar_tensor_tensor(out=zt[b][:, lo:hi], in0=fy[b][:, lo:hi], scalar=negmu[:, b:b + 1],
+                                               in1=gain(lo, hi), op0=ALU.add, op1=ALU.mult)
+
+        def finish(b, edges, queues):
+            for c, (lo, hi) in enumerate(pieces(0, OWN_FROM[b], edges)):
+                nc.vector.scalar_tensor_tensor(out=zt[b][:, lo:hi], in0=zt[b][:, lo:hi], scalar=rstd[:, b:b + 1],
+                                               in1=shift_psum(lo, hi), op0=ALU.mult, op1=ALU.add)
+                queues[c % len(queues)].dma_start(out=out[b, :, lo:hi], in_=zt[b][:, lo:hi])
+
+        def own_share(b):
+            lo = OWN_FROM[b]
+            nc.gpsimd.tensor_scalar(out=gz[b][:], in0=fy[b][:, lo:N], scalar1=negmu[:, b:b + 1],
+                                    scalar2=rstd[:, b:b + 1], op0=ALU.add, op1=ALU.mult)
+            nc.gpsimd.tensor_tensor(out=gz[b][:], in0=gz[b][:], in1=g_bc[:, lo:N], op=ALU.mult)
+            nc.gpsimd.tensor_tensor(out=gz[b][:], in0=gz[b][:], in1=b_bc[:, lo:N], op=ALU.add)
+
+        def store_own_share(b, queue):
+            queue.dma_start(out=out[b, :, OWN_FROM[b]:N], in_=gz[b][:])
 
         mean(0)
-        y_bank(1, 1)
         mean(1)
-        y_bank(0, 2)
-        y_bank(1, 2)
-        mean(2)
         spread(0)
         y_bank(0, 3)
+        y_bank(1, 2)
+        mean(2)
         y_bank(1, 3)
         mean(3)
+        b_bank = spread_columns(acc_pool, "acc", list(range(12, 20)))
+        g_bank = spread_columns(tp_pool, "tp", list(range(0, 8)))
+        rest_bank = spread_columns(acc_pool, "acc", list(range(8, 12)) + list(range(20, 24)))
         spread(1)
         spread(2)
         spread(3)
-        centre(0)
-        centre(1)
-        centre(2)
-        finish(0)
-        centre(3)
-        finish(1)
-        finish(2)
-        finish(3)
+
+        def gain_sbuf(lo, hi):
+            return g_bc[:, lo:hi]
+
+        def gain_psum(lo, hi):
+            return g_bank[:, lo:hi] if hi <= 1024 else rest_bank[:, lo - 1024:hi - 1024]
+
+        def shift_psum(lo, hi):
+            return b_bank[:, lo:hi] if hi <= 1024 else rest_bank[:, lo - 512:hi - 512]
+
+        centre(0, gain_sbuf)
+        centre(1, gain_sbuf)
+        finish(0, [1024], [nc.sync])
+        own_share(0)
+        store_own_share(0, nc.sync)
+        centre(2, gain_psum)
+        centre(3, gain_psum)
+        finish(1, [1024], [nc.sync])
+        own_share(1)
+        store_own_share(1, nc.scalar)
+        finish(2, [1024], [nc.sync])
+        finish(3, [640, 1024], [nc.sync, nc.scalar])

@@ -21,7 +21,7 @@ N = 1536
 NB = 4
 PASSES = 3
 LN_EPS = 1e-5
-OWN_FROM = [768, 1024, N, N]
+OWN_FROM = [640, 1280, N, N]
 
 
 def tile_hierarchicalattention_pb_kernel(tc, ctx_heads, Wo_bytes, Wo_scale, bo, features, ln_g, ln_b, out):
@@ -48,6 +48,7 @@ def tile_hierarchicalattention_pb_kernel(tc, ctx_heads, Wo_bytes, Wo_scale, bo, 
         gb_rows = const.tile([P, P], BF16, name="gb_rows")
         gb_col = const.tile([P, 24], BF16, name="gb_col")
         gz = [const.tile([P, N - OWN_FROM[b]], F32, name="gz%d" % b) for b in range(2)]
+        own_bias = [const.tile([P, 1], F32, name="own_bias%d" % b) for b in range(2)]
         wo_raw = [const.tile([P, K], U8, name="wo_raw%d" % j) for j in range(12)]
         ctx_sb = [const.tile([P, 2, K], BF16, name="ctx_sb%d" % bp) for bp in range(2)]
         cgrp = const.tile([P, PASSES * 2048], BF16, name="cgrp", align_bytes=64)
@@ -90,6 +91,8 @@ def tile_hierarchicalattention_pb_kernel(tc, ctx_heads, Wo_bytes, Wo_scale, bo, 
             load_wo(j)
         load_ctx(1)
         load_wo(5)
+        nc.sync.dma_start(out=gb_rows[0:12, :], in_=ln_g.rearrange("(j p) -> j p", p=P))
+        nc.sync.dma_start(out=gb_rows[12:24, :], in_=ln_b.rearrange("(j p) -> j p", p=P))
         nc.sync.dma_start(out=feat_last[:], in_=features[:, :, 1024:N].rearrange("b s f -> s b f"))
         for j in range(6, 8):
             load_wo(j)
@@ -97,8 +100,6 @@ def tile_hierarchicalattention_pb_kernel(tc, ctx_heads, Wo_bytes, Wo_scale, bo, 
             nc.sync.dma_start(out=feat[b][:], in_=features[b][:, 0:1024])
         for j in range(8, 12):
             load_wo(j)
-        nc.sync.dma_start(out=gb_rows[0:12, :], in_=ln_g.rearrange("(j p) -> j p", p=P))
-        nc.sync.dma_start(out=gb_rows[12:24, :], in_=ln_b.rearrange("(j p) -> j p", p=P))
         nc.sync.dma_start(out=g_bc[:], in_=ln_g.partition_broadcast(P))
         nc.sync.dma_start(out=b_bc[:], in_=ln_b.partition_broadcast(P))
         make_identity(nc, ident[:])
@@ -190,13 +191,17 @@ def tile_hierarchicalattention_pb_kernel(tc, ctx_heads, Wo_bytes, Wo_scale, bo, 
         def add_transposed(bank, cols, in_, last):
             nc.tensor.matmul(out=bank[:, cols], lhsT=in_, rhs=ident[:], is_transpose=True, start=False, stop=last)
 
-        def y_bank(J, b):
-            ybank = y_pool.tile([P, 512], F32, name="yps", tag="yps")
+        def y_bank(J, b, by_vector=False, pool=None, tag="yps"):
+            ybank = (pool or y_pool).tile([P, 512], F32, name=tag, tag=tag)
             nc.tensor.matmul(out=ybank[:], lhsT=ident_bf[:], rhs=feat[b][:, 512 * J:512 * (J + 1)], start=True, stop=False)
             for i in range(4):
                 add_transposed(ybank, slice(P * i, P * (i + 1)), a_t[4 * J + i][:, P * b:P * (b + 1)], i == 3)
-            nc.scalar.activation(out=fy[b][:, 512 * J:512 * (J + 1)], in_=ybank[:], func=ACT.Copy,
-                                 accum_out=sums[:, b, J:J + 1])
+            if by_vector:
+                nc.vector.tensor_scalar(out=fy[b][:, 512 * J:512 * (J + 1)], in0=ybank[:], scalar1=1.0, scalar2=0.0,
+                                        op0=ALU.mult, op1=ALU.add, accum_out=sums[:, b, J:J + 1])
+            else:
+                nc.scalar.activation(out=fy[b][:, 512 * J:512 * (J + 1)], in_=ybank[:], func=ACT.Copy,
+                                     accum_out=sums[:, b, J:J + 1])
 
         def spread_bo():
             bank = y_pool.tile([P, 512], F32, name="yps", tag="yps")
@@ -278,6 +283,7 @@ def tile_hierarchicalattention_pb_kernel(tc, ctx_heads, Wo_bytes, Wo_scale, bo, 
         keep_busy()
         grps[2] = wo_turn(w)
         keep_busy()
+        turn_gain_shift()
         spread_bo()
         wo_quant(1, grps[1], both)
         ctx_quant()
@@ -293,19 +299,16 @@ def tile_hierarchicalattention_pb_kernel(tc, ctx_heads, Wo_bytes, Wo_scale, bo, 
         w = new_pair()
         widen(4, w, [(0, None), (1, None)])
         grps[4] = wo_turn(w)
-        turn_gain_shift()
         wo_quant(3, grps[3], both)
         product(3)
         w = new_pair()
         widen(5, w, [(i, g) for g in range(PASSES) for i in range(2)])
         grps[5] = wo_turn(w)
         y_bank(1, 0)
-        y_bank(1, 1)
         features_and_bo(0)
         features_and_bo(1)
         wo_quant(4, grps[4], both)
         banks4 = product_tokens(4, acc_pool, "acc")
-        y_bank(0, 2)
         features_and_bo(2)
         features_and_bo(3)
         wo_quant(5, grps[5], both)
@@ -330,8 +333,8 @@ def tile_hierarchicalattention_pb_kernel(tc, ctx_heads, Wo_bytes, Wo_scale, bo, 
             cuts = [lo] + [e for e in edges if lo < e < hi] + [hi]
             return [(cuts[i], cuts[i + 1]) for i in range(len(cuts) - 1)]
 
-        def centre(b, gain):
-            for lo, hi in pieces(0, OWN_FROM[b], [1024]):
+        def centre(b, gain, edges):
+            for lo, hi in pieces(0, OWN_FROM[b], edges):
                 nc.vector.scalar_tensor_tensor(out=zt[b][:, lo:hi], in0=fy[b][:, lo:hi], scalar=negmu[:, b:b + 1],
                                                in1=gain(lo, hi), op0=ALU.add, op1=ALU.mult)
 
@@ -343,28 +346,14 @@ def tile_hierarchicalattention_pb_kernel(tc, ctx_heads, Wo_bytes, Wo_scale, bo, 
 
         def own_share(b):
             lo = OWN_FROM[b]
-            nc.gpsimd.tensor_scalar(out=gz[b][:], in0=fy[b][:, lo:N], scalar1=negmu[:, b:b + 1],
-                                    scalar2=rstd[:, b:b + 1], op0=ALU.add, op1=ALU.mult)
+            nc.gpsimd.tensor_tensor(out=own_bias[b][:], in0=negmu[:, b:b + 1], in1=rstd[:, b:b + 1], op=ALU.mult)
+            nc.gpsimd.tensor_scalar(out=gz[b][:], in0=fy[b][:, lo:N], scalar1=rstd[:, b:b + 1], scalar2=own_bias[b][:],
+                                    op0=ALU.mult, op1=ALU.add)
             nc.gpsimd.tensor_tensor(out=gz[b][:], in0=gz[b][:], in1=g_bc[:, lo:N], op=ALU.mult)
             nc.gpsimd.tensor_tensor(out=gz[b][:], in0=gz[b][:], in1=b_bc[:, lo:N], op=ALU.add)
 
         def store_own_share(b, queue):
             queue.dma_start(out=out[b, :, OWN_FROM[b]:N], in_=gz[b][:])
-
-        mean(0)
-        mean(1)
-        spread(0)
-        y_bank(0, 3)
-        y_bank(1, 2)
-        mean(2)
-        y_bank(1, 3)
-        mean(3)
-        b_bank = spread_columns(acc_pool, "acc", list(range(12, 20)))
-        g_bank = spread_columns(tp_pool, "tp", list(range(0, 8)))
-        rest_bank = spread_columns(acc_pool, "acc", list(range(8, 12)) + list(range(20, 24)))
-        spread(1)
-        spread(2)
-        spread(3)
 
         def gain_sbuf(lo, hi):
             return g_bc[:, lo:hi]
@@ -375,15 +364,31 @@ def tile_hierarchicalattention_pb_kernel(tc, ctx_heads, Wo_bytes, Wo_scale, bo, 
         def shift_psum(lo, hi):
             return b_bank[:, lo:hi] if hi <= 1024 else rest_bank[:, lo - 512:hi - 512]
 
-        centre(0, gain_sbuf)
-        centre(1, gain_sbuf)
+        mean(0)
+        centre(0, gain_sbuf, [])
+        y_bank(1, 1)
+        mean(1)
+        centre(1, gain_sbuf, [])
+        spread(0)
+        y_bank(0, 2)
+        y_bank(1, 2)
+        y_bank(0, 3, by_vector=True, pool=tp_pool, tag="tp")
+        y_bank(1, 3, by_vector=True, pool=acc_pool, tag="acc")
+        b_bank = spread_columns(acc_pool, "acc", list(range(12, 20)))
+        g_bank = spread_columns(tp_pool, "tp", list(range(0, 8)))
+        rest_bank = spread_columns(tp_pool, "tp", list(range(8, 12)) + list(range(20, 24)))
+        mean(2)
+        mean(3)
+        spread(1)
+        spread(2)
+        spread(3)
         finish(0, [1024], [nc.sync])
         own_share(0)
-        store_own_share(0, nc.sync)
-        centre(2, gain_psum)
-        centre(3, gain_psum)
+        centre(2, gain_psum, [1024])
+        centre(3, gain_psum, [1024])
         finish(1, [1024], [nc.sync])
+        store_own_share(0, nc.sync)
         own_share(1)
-        store_own_share(1, nc.scalar)
         finish(2, [1024], [nc.sync])
-        finish(3, [640, 1024], [nc.sync, nc.scalar])
+        store_own_share(1, nc.sync)
+        finish(3, [640, 1024, 1280], [nc.sync, nc.scalar])

@@ -213,9 +213,9 @@ def tile_hierarchicalattention_pb_kernel(tc, ctx_heads, Wo_bytes, Wo_scale, bo, 
         def features_and_bo(b):
             nc.vector.tensor_tensor(out=fb[b][:], in0=feat_last[:, b, :], in1=bo_bc[:], op=ALU.add)
 
-        def product_tokens(q, pool, tag):
+        def product_tokens(q, pool, tag, halves=(0, 1)):
             banks = []
-            for half in range(2):
+            for half in halves:
                 bank = pool.tile([P, 512], F32, name=tag, tag=tag)
                 banks.append(bank)
                 for b in (2 * half, 2 * half + 1):
@@ -312,10 +312,12 @@ def tile_hierarchicalattention_pb_kernel(tc, ctx_heads, Wo_bytes, Wo_scale, bo, 
         features_and_bo(2)
         features_and_bo(3)
         wo_quant(5, grps[5], both)
-        banks5 = product_tokens(5, tp_pool, "tp")
+        banks5 = product_tokens(5, tp_pool, "tp", halves=(0,))
+        y_bank(1, 1)
+        banks5 = banks5 + product_tokens(5, tp_pool, "tp", halves=(1,))
         for b in range(NB):
             add_tokens(4, b, banks4)
-        for b in range(NB):
+        for b in range(2):
             add_tokens(5, b, banks5)
 
 
@@ -365,15 +367,16 @@ def tile_hierarchicalattention_pb_kernel(tc, ctx_heads, Wo_bytes, Wo_scale, bo, 
             return b_bank[:, lo:hi] if hi <= 1024 else rest_bank[:, lo - 512:hi - 512]
 
         mean(0)
-        centre(0, gain_sbuf, [])
-        y_bank(1, 1)
         mean(1)
+        centre(0, gain_sbuf, [])
+        for b in range(2, NB):
+            add_tokens(5, b, banks5)
         centre(1, gain_sbuf, [])
         spread(0)
         y_bank(0, 2)
         y_bank(1, 2)
         y_bank(0, 3, by_vector=True, pool=tp_pool, tag="tp")
-        y_bank(1, 3, by_vector=True, pool=acc_pool, tag="acc")
+        y_bank(1, 3, pool=acc_pool, tag="acc")
         b_bank = spread_columns(acc_pool, "acc", list(range(12, 20)))
         g_bank = spread_columns(tp_pool, "tp", list(range(0, 8)))
         rest_bank = spread_columns(tp_pool, "tp", list(range(8, 12)) + list(range(20, 24)))

@@ -375,13 +375,13 @@ def tile_hierarchicalattention_pb_kernel(tc, ctx_heads, Wo_bytes, Wo_scale, bo, 
         spread(0)
         y_bank(0, 2)
         y_bank(1, 2)
+        mean(2)
         y_bank(0, 3, by_vector=True, pool=tp_pool, tag="tp")
-        y_bank(1, 3, pool=acc_pool, tag="acc")
         b_bank = spread_columns(acc_pool, "acc", list(range(12, 20)))
+        y_bank(1, 3, pool=acc_pool, tag="acc")
+        mean(3)
         g_bank = spread_columns(tp_pool, "tp", list(range(0, 8)))
         rest_bank = spread_columns(tp_pool, "tp", list(range(8, 12)) + list(range(20, 24)))
-        mean(2)
-        mean(3)
         spread(1)
         spread(2)
         spread(3)

from contextlib import ExitStack

import concourse.mybir as mybir
from concourse.masks import make_identity

FLOPS = 2 * 512 * 1536 * 1536

F32 = mybir.dt.float32
BF16 = mybir.dt.bfloat16
U32 = mybir.dt.uint32
U8 = mybir.dt.uint8
FP8 = mybir.dt.float8_e4m3fn
FP8X4 = mybir.dt.float8_e4m3fn_x4
ALU = mybir.AluOpType
ACT = mybir.ActivationFunctionType
AX = mybir.AxisListType

P = 128
K = 1536
N = 1536
NB = 4
PASSES = 3
LN_EPS = 1e-5
OWN_FROM = [640, 1280, N, N]


def tile_hierarchicalattention_pb_kernel(tc, ctx_heads, Wo_bytes, Wo_scale, bo, features, ln_g, ln_b, out):
    nc = tc.nc
    with ExitStack() as es:
        const = es.enter_context(tc.tile_pool(name="const", bufs=1))
        wbf_pool = es.enter_context(tc.tile_pool(name="wbf", bufs=6))
        grp_pool = es.enter_context(tc.tile_pool(name="grp", bufs=3))
        tp_pool = es.enter_context(tc.psum_pool(name="tp", bufs=3))
        acc_pool = es.enter_context(tc.psum_pool(name="acc", bufs=2))
        y_pool = es.enter_context(tc.psum_pool(name="yps", bufs=3))
        es.enter_context(tc.manual_schedule())

        ident = const.tile([P, P], F32, name="ident")
        warm = const.tile([P, 1], F32, name="warm")
        ident_bf = const.tile([P, P], BF16, name="ident_bf")
        scale_col = const.tile([P, 12], F32, name="scale_col")
        scale_bc = const.tile([P, K], F32, name="scale_bc")
        bo_rows = const.tile([P, P], BF16, name="bo_rows")
        bo_col = const.tile([P, 12], F32, name="bo_col")
        bo_bc = const.tile([P, 512], F32, name="bo_bc")
        g_bc = const.tile([P, N], BF16, name="g_bc")
        b_bc = const.tile([P, N], BF16, name="b_bc")
        gb_rows = const.tile([P, P], BF16, name="gb_rows")
        gb_col = const.tile([P, 24], BF16, name="gb_col")
        gz = [const.tile([P, N - OWN_FROM[b]], F32, name="gz%d" % b) for b in range(2)]
        own_bias = [const.tile([P, 1], F32, name="own_bias%d" % b) for b in range(2)]
        wo_raw = [const.tile([P, K], U8, name="wo_raw%d" % j) for j in range(12)]
        ctx_sb = [const.tile([P, 2, K], BF16, name="ctx_sb%d" % bp) for bp in range(2)]
        cgrp = const.tile([P, PASSES * 2048], BF16, name="cgrp", align_bytes=64)
        ctx_codes = const.tile([P, PASSES * 512], U32, name="ctx_codes", align_bytes=64)
        ctx_sc = const.tile([P, PASSES * 512], U8, name="ctx_sc", align_bytes=64)
        wo_codes = [[const.tile([P, 256 * w], U32, name="wo_codes%d_%d" % (q, w), align_bytes=64) for w in (2, 1)]
                    for q in range(6)]
        wo_sc = [[const.tile([P, 256 * w], U8, name="wo_sc%d_%d" % (q, w), align_bytes=64) for w in (2, 1)]
                 for q in range(6)]
        a_t = [const.tile([P, 512], F32, name="a_t%d" % j) for j in range(8)]
        feat = [const.tile([P, 1024], BF16, name="feat%d" % b) for b in range(NB)]
        feat_last = const.tile([P, NB, 512], BF16, name="feat_last")
        fb = [const.tile([P, 512], F32, name="fb%d" % b) for b in range(NB)]
        fy = [const.tile([P, N], F32, name="fy%d" % b) for b in range(NB)]
        zt = [const.tile([P, N], F32, name="zt%d" % b) for b in range(NB)]
        junk = const.tile([P, N], BF16, name="junk")
        sums = const.tile([P, NB, 4], F32, name="sums")
        tot = const.tile([P, NB, 4], F32, name="tot")
        negmu = const.tile([P, NB], F32, name="negmu")
        ssq = const.tile([P, NB], F32, name="ssq")
        rstd = const.tile([P, NB], F32, name="rstd")

        def load_wo(j):
            nc.sync.dma_start(out=wo_raw[j][:], in_=Wo_bytes[P * j:P * (j + 1), :])

        def load_ctx(bp):
            nc.sync.dma_start(out=ctx_sb[bp][:].rearrange("p b (h d) -> p (b h) d", h=12),
                              in_=ctx_heads[2 * bp:2 * bp + 2].rearrange("b h s d -> s (b h) d"))

        nc.gpsimd.memset(bo_rows[:], 0.0)
        nc.gpsimd.memset(gb_rows[:], 0.0)
        with nc.allow_non_contiguous_dma(reason="four scales in a row to a partition, three times"):
            nc.sync.dma_start(out=scale_col[:].rearrange("p (g t) -> p g t", t=4),
                              in_=Wo_scale.rearrange("o (g p t) -> p (o g) t", p=P, t=4))
        load_wo(0)
        load_wo(1)
        nc.sync.dma_start(out=bo_rows[0:12, :], in_=bo.rearrange("(j p) -> j p", p=P))
        load_ctx(0)
        for j in range(2, 5):
            load_wo(j)
        load_ctx(1)
        load_wo(5)
        nc.sync.dma_start(out=gb_rows[0:12, :], in_=ln_g.rearrange("(j p) -> j p", p=P))
        nc.sync.dma_start(out=gb_rows[12:24, :], in_=ln_b.rearrange("(j p) -> j p", p=P))
        nc.sync.dma_start(out=feat_last[:], in_=features[:, :, 1024:N].rearrange("b s f -> s b f"))
        for j in range(6, 8):
            load_wo(j)
        for b in range(NB):
            nc.sync.dma_start(out=feat[b][:], in_=features[b][:, 0:1024])
        for j in range(8, 12):
            load_wo(j)
        nc.sync.dma_start(out=g_bc[:], in_=ln_g.partition_broadcast(P))
        nc.sync.dma_start(out=b_bc[:], in_=ln_b.partition_broadcast(P))
        make_identity(nc, ident[:])
        make_identity(nc, ident_bf[:])
        nc.vector.memset(warm[:], 1.0)
        nc.scalar.activation(out=warm[:], in_=warm[:], func=ACT.Abs_reciprocal_sqrt)

        def keep_busy():
            scratch = y_pool.tile([P, 512], F32, name="yps", tag="yps")
            nc.tensor.matmul(out=scratch[:, 0:256], lhsT=ident[:], rhs=scale_bc[:, 0:256], start=True, stop=True)

        def new_pair():
            two = [wbf_pool.tile([P, K], BF16, name="wbf", tag="wbf") for i in range(2)]
            return [two[0][:], two[1][:]]

        def widen(q, two, pieces):
            for i, g in pieces:
                cols = slice(0, K) if g is None else slice(512 * g, 512 * (g + 1))
                nc.vector.tensor_tensor(out=two[i][:, cols], in0=wo_raw[2 * q + i][:, cols].bitcast(FP8),
                                        in1=scale_bc[:, cols], op=ALU.mult)

        def turn_bank(two, g):
            bank = tp_pool.tile([P, 2, 2, P], F32, name="tp", tag="tp")
            for i in range(2):
                words = two[i].bitcast(F32)
                for u in range(2):
                    nc.tensor.transpose(out=bank[:, i, u, :], in_=words[:, 256 * g + u:256 * (g + 1):2],
                                        identity=ident[:])
            return bank

        def turn(two):
            return [turn_bank(two, g) for g in range(PASSES)]

        def copy_out(bank, dst_words):
            nc.scalar.copy(out=dst_words.rearrange("p (i r u) -> p i r u", i=2, u=2),
                           in_=bank[:].rearrange("p i u r -> p i r u"))

        def ctx_turn(bp):
            banks = turn([ctx_sb[bp][:, 0, :], ctx_sb[bp][:, 1, :]])
            for g in range(PASSES):
                copy_out(banks[g], cgrp[:].bitcast(F32)[:, 1024 * g + 512 * bp:1024 * g + 512 * (bp + 1)])

        def ctx_quant():
            for lo, hi in ((0, 2), (2, 3)):
                nc.vector.quantize_mx(out=ctx_codes[:, 512 * lo:512 * hi].bitcast(FP8X4),
                                      scales=ctx_sc[:, 512 * lo:512 * hi], in_=cgrp[:, 2048 * lo:2048 * hi])

        def new_grp():
            return [grp_pool.tile([P, 2048], BF16, name="grp_a", tag="grp_a", align_bytes=64),
                    grp_pool.tile([P, 1024], BF16, name="grp_b", tag="grp_b", align_bytes=64)]

        def wo_turn_pass(two, grp, g):
            bank = turn_bank(two, g)
            copy_out(bank, grp[g // 2][:].bitcast(F32)[:, 512 * (g % 2):512 * (g % 2 + 1)])

        def wo_turn(two):
            grp = new_grp()
            for g in range(PASSES):
                wo_turn_pass(two, grp, g)
            return grp

        def wo_quant(q, grp, parts):
            for part in parts:
                nc.vector.quantize_mx(out=wo_codes[q][part][:].bitcast(FP8X4), scales=wo_sc[q][part][:],
                                      in_=grp[part][:])

        def new_accs():
            return [acc_pool.tile([P, 512], F32, name="acc", tag="acc") for i in range(2)]

        def multiply(q, accs, steps):
            for i, g in steps:
                rows = slice(256 * (g % 2) + P * i, 256 * (g % 2) + P * (i + 1))
                toks = slice(512 * g, 512 * (g + 1))
                nc.tensor.matmul_mx(out=accs[i][:],
                                    lhsT=wo_codes[q][g // 2][:, rows].bitcast(FP8X4),
                                    lhsT_scale=wo_sc[q][g // 2][:, rows],
                                    rhs=ctx_codes[:, toks].bitcast(FP8X4), rhs_scale=ctx_sc[:, toks],
                                    start=(g == 0), stop=(g == PASSES - 1))

        def evacuate_one(q, accs, i):
            j = 2 * q + i
            nc.scalar.activation(out=a_t[j][:], in_=accs[i][:], func=ACT.Identity, bias=bo_col[:, j:j + 1],
                                 scale=1.0)

        def evacuate(q, accs):
            for i in range(2):
                evacuate_one(q, accs, i)

        def add_transposed(bank, cols, in_, last):
            nc.tensor.matmul(out=bank[:, cols], lhsT=in_, rhs=ident[:], is_transpose=True, start=False, stop=last)

        def y_bank(J, b, by_vector=False, pool=None, tag="yps"):
            ybank = (pool or y_pool).tile([P, 512], F32, name=tag, tag=tag)
            nc.tensor.matmul(out=ybank[:], lhsT=ident_bf[:], rhs=feat[b][:, 512 * J:512 * (J + 1)], start=True, stop=False)
            for i in range(4):
                add_transposed(ybank, slice(P * i, P * (i + 1)), a_t[4 * J + i][:, P * b:P * (b + 1)], i == 3)
            if by_vector:
                nc.vector.tensor_scalar(out=fy[b][:, 512 * J:512 * (J + 1)], in0=ybank[:], scalar1=1.0, scalar2=0.0,
                                        op0=ALU.mult, op1=ALU.add, accum_out=sums[:, b, J:J + 1])
            else:
                nc.scalar.activation(out=fy[b][:, 512 * J:512 * (J + 1)], in_=ybank[:], func=ACT.Copy,
                                     accum_out=sums[:, b, J:J + 1])

        def spread_bo():
            bank = y_pool.tile([P, 512], F32, name="yps", tag="yps")
            for i in range(4):
                nc.tensor.transpose(out=bank[:, P * i:P * (i + 1)], in_=bo_col[:, 8 + i:9 + i].to_broadcast([P, P]),
                                    identity=ident[:])
            nc.scalar.copy(out=bo_bc[:], in_=bank[:])

        def features_and_bo(b):
            nc.vector.tensor_tensor(out=fb[b][:], in0=feat_last[:, b, :], in1=bo_bc[:], op=ALU.add)

        def product_tokens(q, pool, tag, halves=(0, 1)):
            banks = []
            for half in halves:
                bank = pool.tile([P, 512], F32, name=tag, tag=tag)
                banks.append(bank)
                for b in (2 * half, 2 * half + 1):
                    for g in range(PASSES):
                        toks = slice(512 * g + P * b, 512 * g + P * (b + 1))
                        rows = slice(256 * (g % 2), 256 * (g % 2 + 1))
                        nc.tensor.matmul_mx(out=bank[:, 256 * (b % 2):256 * (b % 2 + 1)],
                                            lhsT=ctx_codes[:, toks].bitcast(FP8X4), lhsT_scale=ctx_sc[:, toks],
                                            rhs=wo_codes[q][g // 2][:, rows].bitcast(FP8X4),
                                            rhs_scale=wo_sc[q][g // 2][:, rows],
                                            start=(g == 0), stop=(g == PASSES - 1))
            return banks

        def add_tokens(q, b, banks):
            nc.vector.scalar_tensor_tensor(out=fy[b][:, 256 * q:256 * (q + 1)],
                                           in0=banks[b // 2][:, 256 * (b % 2):256 * (b % 2 + 1)], scalar=1.0,
                                           in1=fb[b][:, 256 * (q - 4):256 * (q - 3)],
                                           op0=ALU.mult, op1=ALU.add, accum_out=sums[:, b, q - 2:q - 1])

        def turn_gain_shift():
            turned = y_pool.tile([P, P], BF16, name="yps", tag="yps")
            nc.tensor.transpose(out=turned[:], in_=gb_rows[:], identity=ident_bf[:])
            nc.scalar.copy(out=gb_col[:], in_=turned[:, 0:24])

        def spread_columns(pool, tag, columns):
            bank = pool.tile([P, 1024], BF16, name=tag, tag=tag)
            for i, j in enumerate(columns):
                nc.tensor.transpose(out=bank[:, P * i:P * (i + 1)], in_=gb_col[:, j:j + 1].to_broadcast([P, P]),
                                    identity=ident_bf[:])
            return bank

        every = [(i, g) for i in range(2) for g in range(PASSES)]
        both = [0, 1]
        grps = {}

        def product(q):
            accs = new_accs()
            multiply(q, accs, every)
            evacuate(q, accs)

        for g in range(PASSES):
            spread_bank = y_pool.tile([P, 4, P], F32, name="yps", tag="yps")
            for t in range(4):
                nc.tensor.transpose(out=spread_bank[:, t, :],
                                    in_=scale_col[:, 4 * g + t:4 * g + t + 1].to_broadcast([P, P]), identity=ident[:])
            nc.scalar.copy(out=scale_bc[:, 512 * g:512 * (g + 1)].rearrange("m (p t) -> m p t", t=4),
                           in_=spread_bank[:].rearrange("m t p -> m p t"))
        w = new_pair()
        widen(0, w, [(i, g) for g in range(PASSES) for i in range(2)])
        grps[0] = wo_turn(w)
        bo_turned = y_pool.tile([P, P], BF16, name="yps", tag="yps")
        nc.tensor.transpose(out=bo_turned[:], in_=bo_rows[:], identity=ident_bf[:])
        nc.scalar.copy(out=bo_col[:], in_=bo_turned[:, 0:12])
        keep_busy()
        ctx_turn(0)
        w = new_pair()
        widen(1, w, [(0, None), (1, None)])
        keep_busy()
        grps[1] = wo_turn(w)
        keep_busy()
        ctx_turn(1)
        wo_quant(0, grps[0], both)
        w = new_pair()
        widen(2, w, [(0, None), (1, None)])
        keep_busy()
        grps[2] = wo_turn(w)
        keep_busy()
        turn_gain_shift()
        spread_bo()
        wo_quant(1, grps[1], both)
        ctx_quant()
        product(0)
        product(1)
        w = new_pair()
        widen(3, w, [(0, None), (1, None)])
        grps[3] = wo_turn(w)
        wo_quant(2, grps[2], both)
        product(2)
        y_bank(0, 0)
        y_bank(0, 1)
        w = new_pair()
        widen(4, w, [(0, None), (1, None)])
        grps[4] = wo_turn(w)
        wo_quant(3, grps[3], both)
        product(3)
        w = new_pair()
        widen(5, w, [(i, g) for g in range(PASSES) for i in range(2)])
        grps[5] = wo_turn(w)
        y_bank(1, 0)
        features_and_bo(0)
        features_and_bo(1)
        wo_quant(4, grps[4], both)
        banks4 = product_tokens(4, acc_pool, "acc")
        features_and_bo(2)
        features_and_bo(3)
        wo_quant(5, grps[5], both)
        banks5 = product_tokens(5, tp_pool, "tp", halves=(0,))
        y_bank(1, 1)
        banks5 = banks5 + product_tokens(5, tp_pool, "tp", halves=(1,))
        for b in range(NB):
            add_tokens(4, b, banks4)
        for b in range(2):
            add_tokens(5, b, banks5)


        def mean(b):
            nc.scalar.activation(out=tot[:, b, :], in_=sums[:, b, :], func=ACT.Copy, scale=-1.0 / N,
                                 accum_out=negmu[:, b:b + 1])

        def spread(b):
            nc.scalar.activation(out=junk[:], in_=fy[b][:], func=ACT.Square, bias=negmu[:, b:b + 1], scale=1.0,
                                 accum_out=ssq[:, b:b + 1])
            nc.scalar.activation(out=rstd[:, b:b + 1], in_=ssq[:, b:b + 1], func=ACT.Abs_reciprocal_sqrt, bias=LN_EPS,
                                 scale=1.0 / N)

        def pieces(lo, hi, edges):
            cuts = [lo] + [e for e in edges if lo < e < hi] + [hi]
            return [(cuts[i], cuts[i + 1]) for i in range(len(cuts) - 1)]

        def centre(b, gain, edges):
            for lo, hi in pieces(0, OWN_FROM[b], edges):
                nc.vector.scalar_tensor_tensor(out=zt[b][:, lo:hi], in0=fy[b][:, lo:hi], scalar=negmu[:, b:b + 1],
                                               in1=gain(lo, hi), op0=ALU.add, op1=ALU.mult)

        def finish(b, edges, queues):
            for c, (lo, hi) in enumerate(pieces(0, OWN_FROM[b], edges)):
                nc.vector.scalar_tensor_tensor(out=zt[b][:, lo:hi], in0=zt[b][:, lo:hi], scalar=rstd[:, b:b + 1],
                                               in1=shift_psum(lo, hi), op0=ALU.mult, op1=ALU.add)
                queues[c % len(queues)].dma_start(out=out[b, :, lo:hi], in_=zt[b][:, lo:hi])

        def own_share(b):
            lo = OWN_FROM[b]
            nc.gpsimd.tensor_tensor(out=own_bias[b][:], in0=negmu[:, b:b + 1], in1=rstd[:, b:b + 1], op=ALU.mult)
            nc.gpsimd.tensor_scalar(out=gz[b][:], in0=fy[b][:, lo:N], scalar1=rstd[:, b:b + 1], scalar2=own_bias[b][:],
                                    op0=ALU.mult, op1=ALU.add)
            nc.gpsimd.tensor_tensor(out=gz[b][:], in0=gz[b][:], in1=g_bc[:, lo:N], op=ALU.mult)
            nc.gpsimd.tensor_tensor(out=gz[b][:], in0=gz[b][:], in1=b_bc[:, lo:N], op=ALU.add)

        def store_own_share(b, queue):
            queue.dma_start(out=out[b, :, OWN_FROM[b]:N], in_=gz[b][:])

        def gain_sbuf(lo, hi):
            return g_bc[:, lo:hi]

        def gain_psum(lo, hi):
            return g_bank[:, lo:hi] if hi <= 1024 else rest_bank[:, lo - 1024:hi - 1024]

        def shift_psum(lo, hi):
            return b_bank[:, lo:hi] if hi <= 1024 else rest_bank[:, lo - 512:hi - 512]

        mean(0)
        mean(1)
        centre(0, gain_sbuf, [])
        for b in range(2, NB):
            add_tokens(5, b, banks5)
        centre(1, gain_sbuf, [])
        spread(0)
        y_bank(0, 2)
        y_bank(1, 2)
        mean(2)
        y_bank(0, 3, by_vector=True, pool=tp_pool, tag="tp")
        b_bank = spread_columns(acc_pool, "acc", list(range(12, 20)))
        y_bank(1, 3, pool=acc_pool, tag="acc")
        mean(3)
        g_bank = spread_columns(tp_pool, "tp", list(range(0, 8)))
        rest_bank = spread_columns(tp_pool, "tp", list(range(8, 12)) + list(range(20, 24)))
        spread(1)
        spread(2)
        spread(3)
        finish(0, [1024], [nc.sync])
        own_share(0)
        centre(2, gain_psum, [1024])
        centre(3, gain_psum, [1024])
        finish(1, [1024], [nc.sync])
        store_own_share(0, nc.sync)
        own_share(1)
        finish(2, [1024], [nc.sync])
        store_own_share(1, nc.sync)
        finish(3, [640, 1024, 1280], [nc.sync, nc.scalar])
